import numpy as np
import ml_dtypes


def mxq(x, axis, fmt="e4m3"):
    dtype, down = {"e4m3": (ml_dtypes.float8_e4m3fn, 7), "e5m2": (ml_dtypes.float8_e5m2, 14)}[fmt]
    v = np.moveaxis(np.asarray(x, np.float32).astype(ml_dtypes.bfloat16).astype(np.float64), axis, -1)
    blocks = v.reshape(v.shape[:-1] + (-1, 32))
    amax = np.abs(blocks).max(-1, keepdims=True)
    byte = np.maximum(np.where(amax > 0, np.frexp(amax)[1] - 1 + 127, 0) - down, 1)
    scale = np.exp2(byte - 127.0)
    codes = (blocks / scale).astype(np.float32).astype(dtype).astype(np.float64)
    return np.moveaxis((codes * scale).reshape(v.shape), -1, axis)


WIDE = False


def mx_kscale(k):
    if not WIDE:
        return np.ones(k)
    levels = np.array([10, -10, 5, -5, 0])
    a = np.random.permutation(np.resize(levels, k // 512 * 4)).reshape(k // 512, 4)
    idx = np.arange(k)
    return np.exp2(a[idx // 512, idx % 128 // 32])


BF16 = ml_dtypes.bfloat16


def bf(x):
    return np.asarray(x, np.float32).astype(BF16)


def f64(x):
    return np.asarray(x).astype(np.float64)


B, I, O, G = 2048, 512, 512, 8
K = I * G


def bspline_basis(d):
    inner = 1.0 - 6.0 * d * d + 6.0 * d * d * d
    outer = 2.0 * (1.0 - d) ** 3
    return np.where(d < 0.5, inner, np.where(d < 1.0, outer, np.zeros_like(d)))


def setup_inputs():
    g = np.linspace(-1.0, 1.0, G)
    s = mx_kscale(I)
    u = s / s.max()
    return {"x_norm": bf(np.tanh(np.random.standard_normal((B, I))) * u),
            "spline_weight": bf(np.random.standard_normal((O, I, G)) / np.sqrt(I)),
            "base_activation": bf(np.random.standard_normal((O, I)) * 4.0 / np.sqrt(I) / u),
            "grid_points": bf(g + 0.1 * (g[1] - g[0]) * np.random.standard_normal(G))}


def reference(x_norm, spline_weight, base_activation, grid_points):
    t = f64(x_norm)
    d = np.abs(t[:, :, None] - f64(grid_points))
    basis = bspline_basis(d)
    spline_out = mxq(basis.reshape(B, K), 1, "e4m3") @ mxq(f64(spline_weight).reshape(O, K), 1, "e4m3").T
    base_out = mxq(t, 1, "e4m3") @ mxq(f64(base_activation), 1, "e4m3").T
    return spline_out + 0.1 * base_out

@@ -1,0 +1,206 @@
+import math
+
+import concourse.mybir as mybir
+from concourse.masks import make_identity
+
+F32 = mybir.dt.float32
+BF16 = mybir.dt.bfloat16
+U32 = mybir.dt.uint32
+U8 = mybir.dt.uint8
+FP8X4 = mybir.dt.float8_e4m3fn_x4
+ACT = mybir.ActivationFunctionType
+ALU = mybir.AluOpType
+
+P = 128
+PACK = 4
+B, I, O, G = 2048, 512, 512, 8
+B_TILES = 4
+CHUNK = B_TILES * P
+N_CHUNKS = B // CHUNK
+O_TILES = O // P
+UNIT = CHUNK * PACK
+N_UNITS = N_CHUNKS * G
+
+FLOPS = 2 * B * O * (I * G + I)
+
+
+def tile_advancedkanlayer_pa_kernel(tc, x_norm, spline_weight, base_activation, grid_points, out):
+    nc = tc.nc
+    with tc.tile_pool(name="keep", bufs=1) as keep, tc.tile_pool(name="tents", bufs=3) as tents, tc.tile_pool(
+        name="work", bufs=2
+    ) as work, tc.tile_pool(name="codes", bufs=3) as codes_pool, tc.tile_pool(
+        name="tenths", bufs=2 * B_TILES
+    ) as tenths, tc.tile_pool(name="totals", bufs=3) as totals, tc.psum_pool(
+        name="psum_t", bufs=2
+    ) as psum_t, tc.psum_pool(name="psum_base", bufs=2) as psum_base, tc.psum_pool(
+        name="psum_acc", bufs=B_TILES
+    ) as psum_acc:
+        ident = keep.tile([P, P], BF16)
+        make_identity(nc, ident[:])
+
+        x_sb = keep.tile([P, B // P, I], BF16)
+        x_rows = x_norm.rearrange("(r p) i -> p r i", p=P)
+        nc.sync.dma_start(out=x_sb[:, 0:B_TILES, :], in_=x_rows[:, 0:B_TILES, :])
+        grid_bf = keep.tile([P, G], BF16)
+        nc.sync.dma_start(out=grid_bf[:], in_=grid_points.partition_broadcast(P))
+        a_sb = keep.tile([P, O_TILES, I], BF16)
+        nc.sync.dma_start(out=a_sb[:], in_=base_activation.rearrange("(s p) i -> p s i", p=P))
+        w_sb = keep.tile([P, O_TILES, PACK, P, G], BF16)
+        for s in range(O_TILES):
+            nc.sync.dma_start(
+                out=w_sb[:, s], in_=spline_weight[s * P : (s + 1) * P].rearrange("o (t q) g -> o t q g", t=PACK)
+            )
+        for c in range(1, N_CHUNKS):
+            nc.sync.dma_start(
+                out=x_sb[:, c * B_TILES : (c + 1) * B_TILES, :], in_=x_rows[:, c * B_TILES : (c + 1) * B_TILES, :]
+            )
+
+        one_minus_g = keep.tile([P, G], F32)
+        nc.vector.tensor_scalar(out=one_minus_g[:], in0=grid_bf[:], scalar1=-1.0, scalar2=1.0, op0=ALU.mult, op1=ALU.add)
+        one_plus_g = keep.tile([P, G], F32)
+        nc.vector.tensor_scalar(out=one_plus_g[:], in0=grid_bf[:], scalar1=1.0, scalar2=None, op0=ALU.add)
+
+        a_grouped = keep.tile([P, O, PACK], BF16, align_bytes=64)
+        a_codes = keep.tile([P, O], U32, align_bytes=64)
+        a_scales = keep.tile([P, O], U8, align_bytes=64)
+        x_grouped = keep.tile([P, B, PACK], BF16, align_bytes=64)
+        x_codes = keep.tile([P, B], U32, align_bytes=64)
+        x_scales = keep.tile([P, B], U8, align_bytes=64)
+        w_codes = keep.tile([P, G, O], U32, align_bytes=64)
+        w_scales = keep.tile([P, G, O], U8, align_bytes=64)
+
+        def transpose_four(blocks, grouped, copy_out):
+            turned = psum_t.tile([P, PACK, P], BF16)
+            for t in range(PACK):
+                nc.tensor.transpose(out=turned[:, t, :], in_=blocks[t], identity=ident[:])
+            copy_out(out=grouped, in_=turned[:].rearrange("p t r -> p r t"))
+
+        def copier(n):
+            return nc.scalar.copy if n % 2 == 0 else nc.vector.tensor_copy
+
+        def prepare_base_weights():
+            for s in range(O_TILES):
+                blocks = [a_sb[:, s, t * P : (t + 1) * P] for t in range(PACK)]
+                transpose_four(blocks, a_grouped[:, s * P : (s + 1) * P, :], copier(s))
+            nc.vector.quantize_mx(
+                out=a_codes[:].bitcast(FP8X4), scales=a_scales[:], in_=a_grouped[:].rearrange("p o t -> p (o t)")
+            )
+
+        def prepare_spline_weights(g):
+            w_grouped = work.tile([P, O, PACK], BF16, align_bytes=64)
+            for s in range(O_TILES):
+                blocks = [w_sb[:, s, t, :, g] for t in range(PACK)]
+                transpose_four(blocks, w_grouped[:, s * P : (s + 1) * P, :], copier(s))
+            nc.vector.quantize_mx(
+                out=w_codes[:, g, :].bitcast(FP8X4),
+                scales=w_scales[:, g, :],
+                in_=w_grouped[:].rearrange("p o t -> p (o t)"),
+            )
+
+        base_tenth = {}
+
+        def prepare_chunk(c):
+            for r in range(c * B_TILES, (c + 1) * B_TILES):
+                blocks = [x_sb[:, r, t * P : (t + 1) * P] for t in range(PACK)]
+                transpose_four(blocks, x_grouped[:, r * P : (r + 1) * P, :], copier(r))
+            chunk = slice(c * CHUNK, (c + 1) * CHUNK)
+            nc.vector.quantize_mx(
+                out=x_codes[:, chunk].bitcast(FP8X4),
+                scales=x_scales[:, chunk],
+                in_=x_grouped[:, chunk, :].rearrange("p b t -> p (b t)"),
+            )
+            for r in range(c * B_TILES, (c + 1) * B_TILES):
+                rows = slice(r * P, (r + 1) * P)
+                base_ps = psum_base.tile([P, O], F32)
+                nc.tensor.matmul_mx(
+                    out=base_ps[:],
+                    lhsT=x_codes[:, rows].bitcast(FP8X4),
+                    lhsT_scale=x_scales[:, rows],
+                    rhs=a_codes[:].bitcast(FP8X4),
+                    rhs_scale=a_scales[:],
+                    start=True,
+                    stop=True,
+                )
+                tenth = tenths.tile([P, O], F32)
+                nc.scalar.mul(out=tenth[:], in_=base_ps[:], mul=0.1)
+                base_tenth[r] = tenth
+
+        live = {}
+        acc = {}
+
+        def stage_tent(u):
+            c, g = divmod(u, G)
+            x_flat = x_grouped[:, c * CHUNK : (c + 1) * CHUNK, :].rearrange("p b t -> p (b t)")
+            y = tents.tile([P, UNIT], F32)
+            nc.scalar.activation(out=y[:], in_=x_flat, func=ACT.Identity, bias=one_plus_g[:, g : g + 1], scale=-1.0)
+            nc.vector.scalar_tensor_tensor(
+                out=y[:], in0=x_flat, scalar=one_minus_g[:, g : g + 1], in1=y[:], op0=ALU.add, op1=ALU.min
+            )
+            live[u] = {"y": y}
+
+        def stage_squares(u):
+            y = live[u]["y"]
+            inner = work.tile([P, UNIT], F32)
+            nc.scalar.activation(out=inner[:], in_=y[:], func=ACT.Square, bias=math.sqrt(6.0), scale=-math.sqrt(6.0))
+            outer = work.tile([P, UNIT], F32)
+            nc.scalar.activation(out=outer[:], in_=y[:], func=ACT.Square, scale=math.sqrt(2.0))
+            live[u]["inner"] = inner
+            live[u]["outer"] = outer
+
+        def stage_cubics(u):
+            y, inner, outer = live[u]["y"], live[u]["inner"], live[u]["outer"]
+            nc.vector.scalar_tensor_tensor(out=inner[:], in0=y[:], scalar=-1.0, in1=inner[:], op0=ALU.mult, op1=ALU.mult)
+            outer_bf = work.tile([P, UNIT], BF16)
+            nc.vector.scalar_tensor_tensor(out=outer_bf[:], in0=y[:], scalar=0.0, in1=outer[:], op0=ALU.max, op1=ALU.mult)
+            basis = work.tile([P, UNIT], BF16, align_bytes=64)
+            nc.scalar.activation(out=basis[:], in_=inner[:], func=ACT.Identity, bias=1.0, scale=1.0)
+            live[u]["outer_bf"] = outer_bf
+            live[u]["basis"] = basis
+
+        def stage_quantise(u):
+            basis, outer_bf = live[u]["basis"], live[u]["outer_bf"]
+            nc.vector.tensor_tensor(out=basis[:], in0=basis[:], in1=outer_bf[:], op=ALU.min)
+            n_codes = codes_pool.tile([P, CHUNK], U32, align_bytes=64)
+            n_scales = codes_pool.tile([P, CHUNK], U8, align_bytes=64)
+            nc.vector.quantize_mx(out=n_codes[:].bitcast(FP8X4), scales=n_scales[:], in_=basis[:])
+            live[u] = {"codes": n_codes, "scales": n_scales}
+
+        def stage_matmul(u):
+            c, g = divmod(u, G)
+            n_codes, n_scales = live[u]["codes"], live[u]["scales"]
+            for r in range(B_TILES):
+                if g == 0:
+                    acc[r] = psum_acc.tile([P, O], F32, name="acc")
+                rows = slice(r * P, (r + 1) * P)
+                nc.tensor.matmul_mx(
+                    out=acc[r][:],
+                    lhsT=n_codes[:, rows].bitcast(FP8X4),
+                    lhsT_scale=n_scales[:, rows],
+                    rhs=w_codes[:, g, :].bitcast(FP8X4),
+                    rhs_scale=w_scales[:, g, :],
+                    start=(g == 0),
+                    stop=(g == G - 1),
+                )
+            if g == G - 1:
+                for r in range(B_TILES):
+                    total = totals.tile([P, O], F32)
+                    nc.vector.tensor_tensor(out=total[:], in0=acc[r][:], in1=base_tenth[c * B_TILES + r][:], op=ALU.add)
+                    first = c * CHUNK + r * P
+                    nc.sync.dma_start(out=out[first : first + P, :], in_=total[:])
+
+        def run(stage, u):
+            if 0 <= u < N_UNITS:
+                stage(u)
+
+        prepare_base_weights()
+        prepare_chunk(0)
+        for k in range(N_UNITS + 3):
+            run(stage_quantise, k - 3)
+            run(stage_matmul, k - 3)
+            run(stage_tent, k)
+            run(stage_squares, k - 1)
+            run(stage_cubics, k - 2)
+            if k < G:
+                prepare_spline_weights(k)
+            if k % G == G // 2 and k // G + 1 < N_CHUNKS:
+                prepare_chunk(k // G + 1)

@@ -69,19 +69,16 @@ def tile_advancedkanlayer_pa_kernel(tc, x_norm, spline_weight, base_activation, 
         w_codes = keep.tile([P, G, O], U32, align_bytes=64)
         w_scales = keep.tile([P, G, O], U8, align_bytes=64)
 
-        def transpose_four(blocks, grouped, copy_out):
+        def transpose_four(blocks, grouped):
             turned = psum_t.tile([P, PACK, P], BF16)
             for t in range(PACK):
                 nc.tensor.transpose(out=turned[:, t, :], in_=blocks[t], identity=ident[:])
-            copy_out(out=grouped, in_=turned[:].rearrange("p t r -> p r t"))
-
-        def copier(n):
-            return nc.scalar.copy if n % 2 == 0 else nc.vector.tensor_copy
+            nc.scalar.copy(out=grouped, in_=turned[:].rearrange("p t r -> p r t"))
 
         def prepare_base_weights():
             for s in range(O_TILES):
                 blocks = [a_sb[:, s, t * P : (t + 1) * P] for t in range(PACK)]
-                transpose_four(blocks, a_grouped[:, s * P : (s + 1) * P, :], copier(s))
+                transpose_four(blocks, a_grouped[:, s * P : (s + 1) * P, :])
             nc.vector.quantize_mx(
                 out=a_codes[:].bitcast(FP8X4), scales=a_scales[:], in_=a_grouped[:].rearrange("p o t -> p (o t)")
             )
@@ -90,7 +87,7 @@ def tile_advancedkanlayer_pa_kernel(tc, x_norm, spline_weight, base_activation, 
             w_grouped = work.tile([P, O, PACK], BF16, align_bytes=64)
             for s in range(O_TILES):
                 blocks = [w_sb[:, s, t, :, g] for t in range(PACK)]
-                transpose_four(blocks, w_grouped[:, s * P : (s + 1) * P, :], copier(s))
+                transpose_four(blocks, w_grouped[:, s * P : (s + 1) * P, :])
             nc.vector.quantize_mx(
                 out=w_codes[:, g, :].bitcast(FP8X4),
                 scales=w_scales[:, g, :],
@@ -102,7 +99,7 @@ def tile_advancedkanlayer_pa_kernel(tc, x_norm, spline_weight, base_activation, 
         def prepare_chunk(c):
             for r in range(c * B_TILES, (c + 1) * B_TILES):
                 blocks = [x_sb[:, r, t * P : (t + 1) * P] for t in range(PACK)]
-                transpose_four(blocks, x_grouped[:, r * P : (r + 1) * P, :], copier(r))
+                transpose_four(blocks, x_grouped[:, r * P : (r + 1) * P, :])
             chunk = slice(c * CHUNK, (c + 1) * CHUNK)
             nc.vector.quantize_mx(
                 out=x_codes[:, chunk].bitcast(FP8X4),
@@ -132,7 +129,12 @@ def tile_advancedkanlayer_pa_kernel(tc, x_norm, spline_weight, base_activation, 
             c, g = divmod(u, G)
             x_flat = x_grouped[:, c * CHUNK : (c + 1) * CHUNK, :].rearrange("p b t -> p (b t)")
             y = tents.tile([P, UNIT], F32)
-            nc.scalar.activation(out=y[:], in_=x_flat, func=ACT.Identity, bias=one_plus_g[:, g : g + 1], scale=-1.0)
+            if g % 3 == 0:
+                nc.vector.tensor_scalar(
+                    out=y[:], in0=x_flat, scalar1=-1.0, scalar2=one_plus_g[:, g : g + 1], op0=ALU.mult, op1=ALU.add
+                )
+            else:
+                nc.scalar.activation(out=y[:], in_=x_flat, func=ACT.Identity, bias=one_plus_g[:, g : g + 1], scale=-1.0)
             nc.vector.scalar_tensor_tensor(
                 out=y[:], in0=x_flat, scalar=one_minus_g[:, g : g + 1], in1=y[:], op0=ALU.add, op1=ALU.min
             )

@@ -18,25 +18,27 @@ B_TILES = 4
 CHUNK = B_TILES * P
 N_CHUNKS = B // CHUNK
 O_TILES = O // P
+CELL = P * PACK
 UNIT = CHUNK * PACK
 N_UNITS = N_CHUNKS * G
+ROOT12 = math.sqrt(12.0)
 
 FLOPS = 2 * B * O * (I * G + I)
 
 
 def tile_advancedkanlayer_pa_kernel(tc, x_norm, spline_weight, base_activation, grid_points, out):
     nc = tc.nc
-    with tc.tile_pool(name="keep", bufs=1) as keep, tc.tile_pool(name="tents", bufs=3) as tents, tc.tile_pool(
+    with tc.tile_pool(name="keep", bufs=1) as keep, tc.tile_pool(name="by_chunk", bufs=2) as by_chunk, tc.tile_pool(
         name="work", bufs=2
-    ) as work, tc.tile_pool(name="codes", bufs=3) as codes_pool, tc.tile_pool(
-        name="tenths", bufs=2 * B_TILES
-    ) as tenths, tc.tile_pool(name="totals", bufs=3) as totals, tc.psum_pool(
-        name="psum_t", bufs=2
-    ) as psum_t, tc.psum_pool(name="psum_base", bufs=2) as psum_base, tc.psum_pool(
+    ) as work, tc.tile_pool(name="work3", bufs=3) as work3, tc.tile_pool(name="tenths", bufs=6) as tenths, tc.psum_pool(
+        name="psum_z", bufs=3
+    ) as psum_z, tc.psum_pool(name="psum_prep", bufs=1) as psum_prep, tc.psum_pool(
         name="psum_acc", bufs=B_TILES
     ) as psum_acc:
         ident = keep.tile([P, P], BF16)
         make_identity(nc, ident[:])
+        ident_f32 = keep.tile([P, P], F32)
+        make_identity(nc, ident_f32[:])
 
         x_sb = keep.tile([P, B // P, I], BF16)
         x_rows = x_norm.rearrange("(r p) i -> p r i", p=P)
@@ -55,60 +57,88 @@ def tile_advancedkanlayer_pa_kernel(tc, x_norm, spline_weight, base_activation, 
                 out=x_sb[:, c * B_TILES : (c + 1) * B_TILES, :], in_=x_rows[:, c * B_TILES : (c + 1) * B_TILES, :]
             )
 
-        one_minus_g = keep.tile([P, G], F32)
-        nc.vector.tensor_scalar(out=one_minus_g[:], in0=grid_bf[:], scalar1=-1.0, scalar2=1.0, op0=ALU.mult, op1=ALU.add)
-        one_plus_g = keep.tile([P, G], F32)
-        nc.vector.tensor_scalar(out=one_plus_g[:], in0=grid_bf[:], scalar1=1.0, scalar2=None, op0=ALU.add)
+        def of_knots(factor, offset, knots=slice(0, G)):
+            columns = keep.tile([P, G], F32, name="columns%d" % len(column_tiles))
+            column_tiles.append(columns)
+            nc.vector.tensor_scalar(
+                out=columns[:, knots], in0=grid_bf[:, knots], scalar1=factor, scalar2=offset, op0=ALU.mult, op1=ALU.add
+            )
+            return columns
+
+        column_tiles = []
+        knot = of_knots(1.0, 0.0)
+        minus_root12_g = of_knots(-ROOT12, 0.0)
+        minus_far = of_knots(-1.0, -1.0)
+        minus_half_far = of_knots(-0.5, -0.5)
+        minus_near = of_knots(-1.0, 1.0)
 
         a_grouped = keep.tile([P, O, PACK], BF16, align_bytes=64)
         a_codes = keep.tile([P, O], U32, align_bytes=64)
         a_scales = keep.tile([P, O], U8, align_bytes=64)
-        x_grouped = keep.tile([P, B, PACK], BF16, align_bytes=64)
-        x_codes = keep.tile([P, B], U32, align_bytes=64)
-        x_scales = keep.tile([P, B], U8, align_bytes=64)
         w_codes = keep.tile([P, G, O], U32, align_bytes=64)
         w_scales = keep.tile([P, G, O], U8, align_bytes=64)
 
-        def transpose_four(blocks, grouped):
-            turned = psum_t.tile([P, PACK, P], BF16)
-            for t in range(PACK):
-                nc.tensor.transpose(out=turned[:, t, :], in_=blocks[t], identity=ident[:])
-            nc.scalar.copy(out=grouped, in_=turned[:].rearrange("p t r -> p r t"))
+        def transpose_eight(blocks, grouped):
+            turned = psum_prep.tile([P, len(blocks), PACK, P], BF16, tag="prep")
+            for j in range(len(blocks)):
+                for t in range(PACK):
+                    nc.tensor.transpose(out=turned[:, j, t, :], in_=blocks[j][t], identity=ident[:])
+            nc.scalar.copy(out=grouped, in_=turned[:].rearrange("p j t r -> p j r t"))
+
+        def transpose_tiles(blocks, grouped):
+            for s in range(0, len(blocks), 2):
+                transpose_eight(
+                    blocks[s : s + 2], grouped[:, s * P : (s + 2) * P, :].rearrange("p (j r) t -> p j r t", j=2)
+                )
 
         def prepare_base_weights():
-            for s in range(O_TILES):
-                blocks = [a_sb[:, s, t * P : (t + 1) * P] for t in range(PACK)]
-                transpose_four(blocks, a_grouped[:, s * P : (s + 1) * P, :])
+            transpose_tiles(
+                [[a_sb[:, s, t * P : (t + 1) * P] for t in range(PACK)] for s in range(O_TILES)], a_grouped[:]
+            )
             nc.vector.quantize_mx(
                 out=a_codes[:].bitcast(FP8X4), scales=a_scales[:], in_=a_grouped[:].rearrange("p o t -> p (o t)")
             )
 
         def prepare_spline_weights(g):
             w_grouped = work.tile([P, O, PACK], BF16, align_bytes=64)
-            for s in range(O_TILES):
-                blocks = [w_sb[:, s, t, :, g] for t in range(PACK)]
-                transpose_four(blocks, w_grouped[:, s * P : (s + 1) * P, :])
+            transpose_tiles([[w_sb[:, s, t, :, g] for t in range(PACK)] for s in range(O_TILES)], w_grouped[:])
             nc.vector.quantize_mx(
                 out=w_codes[:, g, :].bitcast(FP8X4),
                 scales=w_scales[:, g, :],
                 in_=w_grouped[:].rearrange("p o t -> p (o t)"),
             )
 
-        base_tenth = {}
+        x_turned = {}
+        x_halved = {}
 
         def prepare_chunk(c):
-            for r in range(c * B_TILES, (c + 1) * B_TILES):
-                blocks = [x_sb[:, r, t * P : (t + 1) * P] for t in range(PACK)]
-                transpose_four(blocks, x_grouped[:, r * P : (r + 1) * P, :])
-            chunk = slice(c * CHUNK, (c + 1) * CHUNK)
-            nc.vector.quantize_mx(
-                out=x_codes[:, chunk].bitcast(FP8X4),
-                scales=x_scales[:, chunk],
-                in_=x_grouped[:, chunk, :].rearrange("p b t -> p (b t)"),
+            tiles = range(c * B_TILES, (c + 1) * B_TILES)
+            minus_half_x = by_chunk.tile([P, B_TILES, I], F32)
+            engine = nc.vector if c == 0 else nc.gpsimd
+            engine.tensor_scalar(
+                out=minus_half_x[:],
+                in0=x_sb[:, c * B_TILES : (c + 1) * B_TILES, :],
+                scalar1=-0.5,
+                scalar2=0.0,
+                op0=ALU.mult,
+                op1=ALU.add,
             )
-            for r in range(c * B_TILES, (c + 1) * B_TILES):
+            x_halved[c] = minus_half_x
+            x_grouped = by_chunk.tile([P, CHUNK, PACK], BF16, align_bytes=64)
+            transpose_tiles([[x_sb[:, r, t * P : (t + 1) * P] for t in range(PACK)] for r in tiles], x_grouped[:])
+            x_turned[c] = x_grouped
+
+        base_tenth = {}
+
+        def base_product(c):
+            x_codes = by_chunk.tile([P, CHUNK], U32, align_bytes=64)
+            x_scales = by_chunk.tile([P, CHUNK], U8, align_bytes=64)
+            nc.vector.quantize_mx(
+                out=x_codes[:].bitcast(FP8X4), scales=x_scales[:], in_=x_turned[c][:].rearrange("p b t -> p (b t)")
+            )
+            for r in range(B_TILES):
                 rows = slice(r * P, (r + 1) * P)
-                base_ps = psum_base.tile([P, O], F32)
+                base_ps = psum_prep.tile([P, O], F32, tag="prep")
                 nc.tensor.matmul_mx(
                     out=base_ps[:],
                     lhsT=x_codes[:, rows].bitcast(FP8X4),
@@ -120,50 +150,136 @@ def tile_advancedkanlayer_pa_kernel(tc, x_norm, spline_weight, base_activation, 
                 )
                 tenth = tenths.tile([P, O], F32)
                 nc.scalar.mul(out=tenth[:], in_=base_ps[:], mul=0.1)
-                base_tenth[r] = tenth
+                base_tenth[c * B_TILES + r] = tenth
 
         live = {}
         acc = {}
 
-        def stage_tent(u):
+        def x_of(u):
+            return x_turned[u // G][:].rearrange("p b t -> p (b t)")
+
+        def outermost(g):
+            return g == 0 or g == G - 1
+
+        def scalar_makes_inner(u):
+            return u >= G
+
+        def stage_max(u):
             c, g = divmod(u, G)
-            x_flat = x_grouped[:, c * CHUNK : (c + 1) * CHUNK, :].rearrange("p b t -> p (b t)")
-            y = tents.tile([P, UNIT], F32)
-            if g % 3 == 0:
-                nc.vector.tensor_scalar(
-                    out=y[:], in0=x_flat, scalar1=-1.0, scalar2=one_plus_g[:, g : g + 1], op0=ALU.mult, op1=ALU.add
-                )
-            else:
-                nc.scalar.activation(out=y[:], in_=x_flat, func=ACT.Identity, bias=one_plus_g[:, g : g + 1], scale=-1.0)
-            nc.vector.scalar_tensor_tensor(
-                out=y[:], in0=x_flat, scalar=one_minus_g[:, g : g + 1], in1=y[:], op0=ALU.add, op1=ALU.min
+            larger = work.tile([P, B_TILES, I], F32)
+            nc.gpsimd.tensor_scalar(
+                out=larger[:],
+                in0=x_sb[:, c * B_TILES : (c + 1) * B_TILES, :],
+                scalar1=3.0e38,
+                scalar2=knot[:, g : g + 1],
+                op0=ALU.min,
+                op1=ALU.max,
             )
-            live[u] = {"y": y}
+            live[u] = {"larger": larger}
 
-        def stage_squares(u):
-            y = live[u]["y"]
-            inner = work.tile([P, UNIT], F32)
-            nc.scalar.activation(out=inner[:], in_=y[:], func=ACT.Square, bias=math.sqrt(6.0), scale=-math.sqrt(6.0))
-            outer = work.tile([P, UNIT], F32)
-            nc.scalar.activation(out=outer[:], in_=y[:], func=ACT.Square, scale=math.sqrt(2.0))
+        def stage_square(u):
+            g = u % G
+            inner = work3.tile([P, UNIT], F32)
+            nc.scalar.activation(
+                out=inner[:], in_=x_of(u), func=ACT.Square, bias=minus_root12_g[:, g : g + 1], scale=ROOT12
+            )
             live[u]["inner"] = inner
-            live[u]["outer"] = outer
 
-        def stage_cubics(u):
-            y, inner, outer = live[u]["y"], live[u]["inner"], live[u]["outer"]
-            nc.vector.scalar_tensor_tensor(out=inner[:], in0=y[:], scalar=-1.0, in1=inner[:], op0=ALU.mult, op1=ALU.mult)
-            outer_bf = work.tile([P, UNIT], BF16)
-            nc.vector.scalar_tensor_tensor(out=outer_bf[:], in0=y[:], scalar=0.0, in1=outer[:], op0=ALU.max, op1=ALU.mult)
-            basis = work.tile([P, UNIT], BF16, align_bytes=64)
-            nc.scalar.activation(out=basis[:], in_=inner[:], func=ACT.Identity, bias=1.0, scale=1.0)
-            live[u]["outer_bf"] = outer_bf
-            live[u]["basis"] = basis
+        def turn_cell(u, r):
+            z = psum_z.tile([P, PACK, P], F32)
+            for t in range(PACK):
+                features = slice(t * P, (t + 1) * P)
+                for source, first in ((live[u]["larger"], True), (x_halved[u // G], False)):
+                    nc.tensor.matmul(
+                        out=z[:, t, :],
+                        lhsT=source[:, r, features],
+                        rhs=ident_f32[:],
+                        is_transpose=True,
+                        start=first,
+                        stop=not first,
+                    )
+            return z[:].rearrange("p t b -> p b t")
+
+        def stage_products(u):
+            g = u % G
+            inner = live[u]["inner"]
+            cube = work3.tile([P, UNIT], BF16, align_bytes=64)
+            outer = work.tile([P, UNIT], F32)
+            half_y = minus_half_far[:, g : g + 1]
+            pending = []
+            if outermost(g):
+                edge = minus_far if g == 0 else minus_near
+                nc.scalar.activation(out=outer[:], in_=x_of(u), func=ACT.Square, bias=edge[:, g : g + 1], scale=1.0)
+
+            def outer_product(r, z):
+                cell = slice(r * CELL, (r + 1) * CELL)
+                nc.vector.scalar_tensor_tensor(
+                    out=cube[:, cell].rearrange("p (b t) -> p b t", t=PACK),
+                    in0=z,
+                    scalar=half_y,
+                    in1=outer[:, cell].rearrange("p (b t) -> p b t", t=PACK),
+                    op0=ALU.add,
+                    op1=ALU.mult,
+                )
+
+            for r in range(B_TILES):
+                cell = slice(r * CELL, (r + 1) * CELL)
+                z = turn_cell(u, r)
+                if not outermost(g):
+                    nc.scalar.activation(
+                        out=outer[:, cell].rearrange("p (b t) -> p b t", t=PACK),
+                        in_=z,
+                        func=ACT.Square,
+                        bias=minus_far[:, g : g + 1],
+                        scale=2.0,
+                    )
+                nc.vector.scalar_tensor_tensor(
+                    out=inner[:, cell].rearrange("p (b t) -> p b t", t=PACK),
+                    in0=z,
+                    scalar=half_y,
+                    in1=inner[:, cell].rearrange("p (b t) -> p b t", t=PACK),
+                    op0=ALU.add,
+                    op1=ALU.mult,
+                )
+                if not outermost(g):
+                    pending.append((r, z))
+                if len(pending) == 2:
+                    outer_product(*pending.pop(0))
+            for r, z in pending:
+                outer_product(r, z)
+            if outermost(g):
+                nc.vector.scalar_tensor_tensor(
+                    out=cube[:], in0=x_of(u), scalar=edge[:, g : g + 1], in1=outer[:], op0=ALU.add, op1=ALU.mult
+                )
+            live[u]["cube"] = cube
+
+        def stage_affine(u):
+            if scalar_makes_inner(u):
+                basis = work3.tile([P, UNIT], BF16, align_bytes=64)
+                nc.scalar.activation(out=basis[:], in_=live[u]["inner"][:], func=ACT.Identity, bias=1.0, scale=1.0)
+                live[u]["basis"] = basis
+
+        def stage_minimum(u):
+            cube = live[u]["cube"]
+            if scalar_makes_inner(u):
+                basis = live[u]["basis"]
+                nc.vector.tensor_tensor(out=basis[:], in0=basis[:], in1=cube[:], op=ALU.min)
+            else:
+                basis = work3.tile([P, UNIT], BF16, align_bytes=64)
+                nc.vector.scalar_tensor_tensor(
+                    out=basis[:], in0=live[u]["inner"][:], scalar=1.0, in1=cube[:], op0=ALU.add, op1=ALU.min
+                )
+            live[u] = {"basis": basis}
+
+        def stage_clamp(u):
+            cube = live[u]["cube"]
+            factor = {0: -2.0, G - 1: 2.0}.get(u % G, -4.0)
+            nc.vector.tensor_scalar(out=cube[:], in0=cube[:], scalar1=factor, scalar2=0.0, op0=ALU.mult, op1=ALU.max)
 
         def stage_quantise(u):
-            basis, outer_bf = live[u]["basis"], live[u]["outer_bf"]
-            nc.vector.tensor_tensor(out=basis[:], in0=basis[:], in1=outer_bf[:], op=ALU.min)
-            n_codes = codes_pool.tile([P, CHUNK], U32, align_bytes=64)
-            n_scales = codes_pool.tile([P, CHUNK], U8, align_bytes=64)
+            basis = live[u]["basis"]
+            n_codes = work3.tile([P, CHUNK], U32, align_bytes=64)
+            n_scales = work3.tile([P, CHUNK], U8, align_bytes=64)
             nc.vector.quantize_mx(out=n_codes[:].bitcast(FP8X4), scales=n_scales[:], in_=basis[:])
             live[u] = {"codes": n_codes, "scales": n_scales}
 
@@ -185,7 +301,7 @@ def tile_advancedkanlayer_pa_kernel(tc, x_norm, spline_weight, base_activation, 
                 )
             if g == G - 1:
                 for r in range(B_TILES):
-                    total = totals.tile([P, O], F32)
+                    total = work.tile([P, O], F32)
                     nc.vector.tensor_tensor(out=total[:], in0=acc[r][:], in1=base_tenth[c * B_TILES + r][:], op=ALU.add)
                     first = c * CHUNK + r * P
                     nc.sync.dma_start(out=out[first : first + P, :], in_=total[:])
@@ -194,15 +310,23 @@ def tile_advancedkanlayer_pa_kernel(tc, x_norm, spline_weight, base_activation, 
             if 0 <= u < N_UNITS:
                 stage(u)
 
-        prepare_base_weights()
+        run(stage_max, 0)
         prepare_chunk(0)
-        for k in range(N_UNITS + 3):
-            run(stage_quantise, k - 3)
-            run(stage_matmul, k - 3)
-            run(stage_tent, k)
-            run(stage_squares, k - 1)
-            run(stage_cubics, k - 2)
+        run(stage_square, 0)
+        for k in range(N_UNITS + 2):
+            run(stage_max, k + 1)
+            run(stage_products, k)
+            run(stage_affine, k - 1)
+            run(stage_minimum, k - 2)
+            run(stage_clamp, k)
+            run(stage_square, k + 1)
             if k < G:
                 prepare_spline_weights(k)
+            run(stage_quantise, k - 2)
+            run(stage_matmul, k - 2)
+            if k == 1:
+                prepare_base_weights()
+            if k % G == 2 and k // G < N_CHUNKS:
+                base_product(k // G)
             if k % G == G // 2 and k // G + 1 < N_CHUNKS:
                 prepare_chunk(k // G + 1)

@@ -21,6 +21,7 @@ O_TILES = O // P
 CELL = P * PACK
 UNIT = CHUNK * PACK
 N_UNITS = N_CHUNKS * G
+RING = 8 - B_TILES
 ROOT12 = math.sqrt(12.0)
 
 FLOPS = 2 * B * O * (I * G + I)
@@ -30,9 +31,9 @@ def tile_advancedkanlayer_pa_kernel(tc, x_norm, spline_weight, base_activation, 
     nc = tc.nc
     with tc.tile_pool(name="keep", bufs=1) as keep, tc.tile_pool(name="by_chunk", bufs=2) as by_chunk, tc.tile_pool(
         name="work", bufs=2
-    ) as work, tc.tile_pool(name="work3", bufs=3) as work3, tc.tile_pool(name="tenths", bufs=6) as tenths, tc.psum_pool(
-        name="psum_z", bufs=3
-    ) as psum_z, tc.psum_pool(name="psum_prep", bufs=1) as psum_prep, tc.psum_pool(
+    ) as work, tc.tile_pool(name="work3", bufs=3) as work3, tc.tile_pool(name="work4", bufs=4) as work4, tc.tile_pool(name="tenths", bufs=6) as tenths, tc.psum_pool(
+        name="psum_ring", bufs=RING
+    ) as psum_ring, tc.psum_pool(
         name="psum_acc", bufs=B_TILES
     ) as psum_acc:
         ident = keep.tile([P, P], BF16)
@@ -79,40 +80,44 @@ def tile_advancedkanlayer_pa_kernel(tc, x_norm, spline_weight, base_activation, 
         w_scales = keep.tile([P, G, O], U8, align_bytes=64)
 
         def transpose_eight(blocks, grouped):
-            turned = psum_prep.tile([P, len(blocks), PACK, P], BF16, tag="prep")
+            turned = psum_ring.tile([P, len(blocks), PACK, P], BF16, tag="bank")
             for j in range(len(blocks)):
                 for t in range(PACK):
                     nc.tensor.transpose(out=turned[:, j, t, :], in_=blocks[j][t], identity=ident[:])
             nc.scalar.copy(out=grouped, in_=turned[:].rearrange("p j t r -> p j r t"))
 
-        def transpose_tiles(blocks, grouped):
-            for s in range(0, len(blocks), 2):
-                transpose_eight(
-                    blocks[s : s + 2], grouped[:, s * P : (s + 2) * P, :].rearrange("p (j r) t -> p j r t", j=2)
-                )
-
-        def prepare_base_weights():
-            transpose_tiles(
-                [[a_sb[:, s, t * P : (t + 1) * P] for t in range(PACK)] for s in range(O_TILES)], a_grouped[:]
+        def turn_pair(block, s, grouped):
+            transpose_eight(
+                [[block(s + j, t) for t in range(PACK)] for j in range(2)],
+                grouped[:, s * P : (s + 2) * P, :].rearrange("p (j r) t -> p j r t", j=2),
             )
+
+        def turn_base_weights(s):
+            turn_pair(lambda s, t: a_sb[:, s, t * P : (t + 1) * P], s, a_grouped[:])
+
+        def quantise_base_weights():
             nc.vector.quantize_mx(
                 out=a_codes[:].bitcast(FP8X4), scales=a_scales[:], in_=a_grouped[:].rearrange("p o t -> p (o t)")
             )
 
-        def prepare_spline_weights(g):
-            w_grouped = work.tile([P, O, PACK], BF16, align_bytes=64)
-            transpose_tiles([[w_sb[:, s, t, :, g] for t in range(PACK)] for s in range(O_TILES)], w_grouped[:])
+        w_turned = {}
+
+        def turn_spline_weights(g, s):
+            if s == 0:
+                w_turned[g] = work.tile([P, O, PACK], BF16, align_bytes=64, name="w_grouped")
+            turn_pair(lambda s, t: w_sb[:, s, t, :, g], s, w_turned[g][:])
+
+        def quantise_spline_weights(g):
             nc.vector.quantize_mx(
                 out=w_codes[:, g, :].bitcast(FP8X4),
                 scales=w_scales[:, g, :],
-                in_=w_grouped[:].rearrange("p o t -> p (o t)"),
+                in_=w_turned[g][:].rearrange("p o t -> p (o t)"),
             )
 
         x_turned = {}
         x_halved = {}
 
-        def prepare_chunk(c):
-            tiles = range(c * B_TILES, (c + 1) * B_TILES)
+        def halve_chunk(c):
             minus_half_x = by_chunk.tile([P, B_TILES, I], F32)
             engine = nc.vector if c == 0 else nc.gpsimd
             engine.tensor_scalar(
@@ -124,33 +129,40 @@ def tile_advancedkanlayer_pa_kernel(tc, x_norm, spline_weight, base_activation, 
                 op1=ALU.add,
             )
             x_halved[c] = minus_half_x
-            x_grouped = by_chunk.tile([P, CHUNK, PACK], BF16, align_bytes=64)
-            transpose_tiles([[x_sb[:, r, t * P : (t + 1) * P] for t in range(PACK)] for r in tiles], x_grouped[:])
-            x_turned[c] = x_grouped
 
-        base_tenth = {}
+        def turn_chunk(c, s):
+            if s == 0:
+                x_turned[c] = by_chunk.tile([P, CHUNK, PACK], BF16, align_bytes=64, name="x_grouped")
+            turn_pair(lambda s, t: x_sb[:, c * B_TILES + s, t * P : (t + 1) * P], s, x_turned[c][:])
 
-        def base_product(c):
+        x_quantised = {}
+
+        def quantise_chunk(c):
             x_codes = by_chunk.tile([P, CHUNK], U32, align_bytes=64)
             x_scales = by_chunk.tile([P, CHUNK], U8, align_bytes=64)
             nc.vector.quantize_mx(
                 out=x_codes[:].bitcast(FP8X4), scales=x_scales[:], in_=x_turned[c][:].rearrange("p b t -> p (b t)")
             )
-            for r in range(B_TILES):
-                rows = slice(r * P, (r + 1) * P)
-                base_ps = psum_prep.tile([P, O], F32, tag="prep")
-                nc.tensor.matmul_mx(
-                    out=base_ps[:],
-                    lhsT=x_codes[:, rows].bitcast(FP8X4),
-                    lhsT_scale=x_scales[:, rows],
-                    rhs=a_codes[:].bitcast(FP8X4),
-                    rhs_scale=a_scales[:],
-                    start=True,
-                    stop=True,
-                )
-                tenth = tenths.tile([P, O], F32)
-                nc.scalar.mul(out=tenth[:], in_=base_ps[:], mul=0.1)
-                base_tenth[c * B_TILES + r] = tenth
+            x_quantised[c] = (x_codes, x_scales)
+
+        base_tenth = {}
+
+        def base_product(c, r):
+            x_codes, x_scales = x_quantised[c]
+            rows = slice(r * P, (r + 1) * P)
+            base_ps = psum_ring.tile([P, O], F32, tag="bank")
+            nc.tensor.matmul_mx(
+                out=base_ps[:],
+                lhsT=x_codes[:, rows].bitcast(FP8X4),
+                lhsT_scale=x_scales[:, rows],
+                rhs=a_codes[:].bitcast(FP8X4),
+                rhs_scale=a_scales[:],
+                start=True,
+                stop=True,
+            )
+            tenth = tenths.tile([P, O], F32)
+            nc.scalar.mul(out=tenth[:], in_=base_ps[:], mul=0.1)
+            base_tenth[c * B_TILES + r] = tenth
 
         live = {}
         acc = {}
@@ -166,12 +178,14 @@ def tile_advancedkanlayer_pa_kernel(tc, x_norm, spline_weight, base_activation, 
 
         def stage_max(u):
             c, g = divmod(u, G)
+            knot_now = work.tile([P, 1], F32)
+            nc.vector.tensor_copy(out=knot_now[:], in_=knot[:, g : g + 1])
             larger = work.tile([P, B_TILES, I], F32)
             nc.gpsimd.tensor_scalar(
                 out=larger[:],
                 in0=x_sb[:, c * B_TILES : (c + 1) * B_TILES, :],
                 scalar1=3.0e38,
-                scalar2=knot[:, g : g + 1],
+                scalar2=knot_now[:],
                 op0=ALU.min,
                 op1=ALU.max,
             )
@@ -179,14 +193,14 @@ def tile_advancedkanlayer_pa_kernel(tc, x_norm, spline_weight, base_activation, 
 
         def stage_square(u):
             g = u % G
-            inner = work3.tile([P, UNIT], F32)
+            inner = work4.tile([P, UNIT], F32)
             nc.scalar.activation(
                 out=inner[:], in_=x_of(u), func=ACT.Square, bias=minus_root12_g[:, g : g + 1], scale=ROOT12
             )
             live[u]["inner"] = inner
 
         def turn_cell(u, r):
-            z = psum_z.tile([P, PACK, P], F32)
+            z = psum_ring.tile([P, PACK, P], F32, tag="bank")
             for t in range(PACK):
                 features = slice(t * P, (t + 1) * P)
                 for source, first in ((live[u]["larger"], True), (x_halved[u // G], False)):
@@ -198,7 +212,11 @@ def tile_advancedkanlayer_pa_kernel(tc, x_norm, spline_weight, base_activation, 
                         start=first,
                         stop=not first,
                     )
-            return z[:].rearrange("p t b -> p b t")
+            live[u][r] = z[:].rearrange("p t b -> p b t")
+
+        def stage_turn(u):
+            for r in range(B_TILES):
+                turn_cell(u, r)
 
         def stage_products(u):
             g = u % G
@@ -224,7 +242,7 @@ def tile_advancedkanlayer_pa_kernel(tc, x_norm, spline_weight, base_activation, 
 
             for r in range(B_TILES):
                 cell = slice(r * CELL, (r + 1) * CELL)
-                z = turn_cell(u, r)
+                z = live[u][r]
                 if not outermost(g):
                     nc.scalar.activation(
                         out=outer[:, cell].rearrange("p (b t) -> p b t", t=PACK),
@@ -299,6 +317,9 @@ def tile_advancedkanlayer_pa_kernel(tc, x_norm, spline_weight, base_activation, 
                     start=(g == 0),
                     stop=(g == G - 1),
                 )
+
+        def stage_store(u):
+            c, g = divmod(u, G)
             if g == G - 1:
                 for r in range(B_TILES):
                     total = work.tile([P, O], F32)
@@ -310,23 +331,48 @@ def tile_advancedkanlayer_pa_kernel(tc, x_norm, spline_weight, base_activation, 
             if 0 <= u < N_UNITS:
                 stage(u)
 
-        run(stage_max, 0)
-        prepare_chunk(0)
-        run(stage_square, 0)
-        for k in range(N_UNITS + 2):
-            run(stage_max, k + 1)
-            run(stage_products, k)
-            run(stage_affine, k - 1)
-            run(stage_minimum, k - 2)
-            run(stage_clamp, k)
-            run(stage_square, k + 1)
-            if k < G:
-                prepare_spline_weights(k)
-            run(stage_quantise, k - 2)
-            run(stage_matmul, k - 2)
-            if k == 1:
-                prepare_base_weights()
-            if k % G == 2 and k // G < N_CHUNKS:
-                base_product(k // G)
-            if k % G == G // 2 and k // G + 1 < N_CHUNKS:
-                prepare_chunk(k // G + 1)
+        with tc.manual_schedule(
+            engines={
+                mybir.EngineType.PE,
+                mybir.EngineType.Activation,
+                mybir.EngineType.DVE,
+                mybir.EngineType.Pool,
+            }
+        ):
+            halve_chunk(0)
+            stage_max(0)
+            turn_chunk(0, 0)
+            turn_chunk(0, 2)
+            stage_turn(0)
+            stage_square(0)
+            for k in range(N_UNITS + 3):
+                c, step = divmod(k, G)
+                run(stage_max, k + 1)
+                run(stage_products, k)
+                run(stage_store, k - 3)
+                run(stage_square, k + 1)
+                if c == 0:
+                    turn_spline_weights(k, 0)
+                    turn_spline_weights(k, 2)
+                elif step in (4, 5) and c + 1 < N_CHUNKS:
+                    turn_chunk(c + 1, 2 * (step - 4))
+                if k in (1, 2):
+                    turn_base_weights(2 * (k - 1))
+                if c == 0 and step in (5, 6):
+                    turn_chunk(1, 2 * (step - 5))
+                if 4 <= step and c < N_CHUNKS:
+                    base_product(c, step - 4)
+                if c + 1 < N_CHUNKS and step == 4:
+                    halve_chunk(c + 1)
+                run(stage_turn, k + 1)
+                run(stage_affine, k - 1)
+                run(stage_minimum, k - 2)
+                run(stage_clamp, k)
+                if 1 <= k <= G:
+                    quantise_spline_weights(k - 1)
+                if k == 3:
+                    quantise_base_weights()
+                if step == 3 and c < N_CHUNKS:
+                    quantise_chunk(c)
+                run(stage_quantise, k - 2)
+                run(stage_matmul, k - 2)

@@ -22,6 +22,7 @@ CELL = P * PACK
 UNIT = CHUNK * PACK
 N_UNITS = N_CHUNKS * G
 RING = 8 - B_TILES
+HUGE = 3.0e38
 ROOT12 = math.sqrt(12.0)
 
 FLOPS = 2 * B * O * (I * G + I)
@@ -58,20 +59,20 @@ def tile_advancedkanlayer_pa_kernel(tc, x_norm, spline_weight, base_activation, 
                 out=x_sb[:, c * B_TILES : (c + 1) * B_TILES, :], in_=x_rows[:, c * B_TILES : (c + 1) * B_TILES, :]
             )
 
-        def of_knots(factor, offset, knots=slice(0, G)):
+        def of_knots(factor, offset, last_offset):
             columns = keep.tile([P, G], F32, name="columns%d" % len(column_tiles))
             column_tiles.append(columns)
-            nc.vector.tensor_scalar(
-                out=columns[:, knots], in0=grid_bf[:, knots], scalar1=factor, scalar2=offset, op0=ALU.mult, op1=ALU.add
-            )
+            for knots, added in ((slice(0, G - 1), offset), (slice(G - 1, G), last_offset)):
+                nc.vector.tensor_scalar(
+                    out=columns[:, knots], in0=grid_bf[:, knots], scalar1=factor, scalar2=added, op0=ALU.mult, op1=ALU.add
+                )
             return columns
 
         column_tiles = []
-        knot = of_knots(1.0, 0.0)
-        minus_root12_g = of_knots(-ROOT12, 0.0)
-        minus_far = of_knots(-1.0, -1.0)
-        minus_half_far = of_knots(-0.5, -0.5)
-        minus_near = of_knots(-1.0, 1.0)
+        knot = of_knots(1.0, 0.0, 0.0)
+        minus_root12_g = of_knots(-ROOT12, 0.0, 0.0)
+        y_offset = of_knots(-1.0, -1.0, 1.0)
+        half_y_offset = of_knots(-0.5, -0.5, 0.5)
 
         a_grouped = keep.tile([P, O, PACK], BF16, align_bytes=64)
         a_codes = keep.tile([P, O], U32, align_bytes=64)
@@ -170,22 +171,20 @@ def tile_advancedkanlayer_pa_kernel(tc, x_norm, spline_weight, base_activation, 
         def x_of(u):
             return x_turned[u // G][:].rearrange("p b t -> p (b t)")
 
-        def outermost(g):
-            return g == 0 or g == G - 1
-
         def scalar_makes_inner(u):
-            return u >= G
+            return u >= G or u % G == G - 1
 
         def stage_max(u):
             c, g = divmod(u, G)
             knot_now = work.tile([P, 1], F32)
             nc.vector.tensor_copy(out=knot_now[:], in_=knot[:, g : g + 1])
             larger = work.tile([P, B_TILES, I], F32)
+            last = g == G - 1
             nc.gpsimd.tensor_scalar(
                 out=larger[:],
                 in0=x_sb[:, c * B_TILES : (c + 1) * B_TILES, :],
-                scalar1=3.0e38,
-                scalar2=knot_now[:],
+                scalar1=knot_now[:] if last else HUGE,
+                scalar2=-HUGE if last else knot_now[:],
                 op0=ALU.min,
                 op1=ALU.max,
             )
@@ -223,58 +222,38 @@ def tile_advancedkanlayer_pa_kernel(tc, x_norm, spline_weight, base_activation, 
             inner = live[u]["inner"]
             cube = work3.tile([P, UNIT], BF16, align_bytes=64)
             outer = work.tile([P, UNIT], F32)
-            half_y = minus_half_far[:, g : g + 1]
-            pending = []
-            if outermost(g):
-                edge = minus_far if g == 0 else minus_near
-                nc.scalar.activation(out=outer[:], in_=x_of(u), func=ACT.Square, bias=edge[:, g : g + 1], scale=1.0)
 
-            def outer_product(r, z):
+            def product(r, factor, result):
                 cell = slice(r * CELL, (r + 1) * CELL)
                 nc.vector.scalar_tensor_tensor(
-                    out=cube[:, cell].rearrange("p (b t) -> p b t", t=PACK),
-                    in0=z,
-                    scalar=half_y,
-                    in1=outer[:, cell].rearrange("p (b t) -> p b t", t=PACK),
+                    out=result[:, cell].rearrange("p (b t) -> p b t", t=PACK),
+                    in0=live[u][r],
+                    scalar=half_y_offset[:, g : g + 1],
+                    in1=factor[:, cell].rearrange("p (b t) -> p b t", t=PACK),
                     op0=ALU.add,
                     op1=ALU.mult,
                 )
 
             for r in range(B_TILES):
-                cell = slice(r * CELL, (r + 1) * CELL)
-                z = live[u][r]
-                if not outermost(g):
-                    nc.scalar.activation(
-                        out=outer[:, cell].rearrange("p (b t) -> p b t", t=PACK),
-                        in_=z,
-                        func=ACT.Square,
-                        bias=minus_far[:, g : g + 1],
-                        scale=2.0,
-                    )
-                nc.vector.scalar_tensor_tensor(
-                    out=inner[:, cell].rearrange("p (b t) -> p b t", t=PACK),
-                    in0=z,
-                    scalar=half_y,
-                    in1=inner[:, cell].rearrange("p (b t) -> p b t", t=PACK),
-                    op0=ALU.add,
-                    op1=ALU.mult,
+                nc.scalar.activation(
+                    out=outer[:, r * CELL : (r + 1) * CELL].rearrange("p (b t) -> p b t", t=PACK),
+                    in_=live[u][r],
+                    func=ACT.Square,
+                    bias=y_offset[:, g : g + 1],
+                    scale=2.0,
                 )
-                if not outermost(g):
-                    pending.append((r, z))
-                if len(pending) == 2:
-                    outer_product(*pending.pop(0))
-            for r, z in pending:
-                outer_product(r, z)
-            if outermost(g):
-                nc.vector.scalar_tensor_tensor(
-                    out=cube[:], in0=x_of(u), scalar=edge[:, g : g + 1], in1=outer[:], op0=ALU.add, op1=ALU.mult
-                )
+            for r in range(B_TILES + 1):
+                if r < B_TILES:
+                    product(r, inner, inner)
+                if r > 0:
+                    product(r - 1, outer, cube)
             live[u]["cube"] = cube
 
         def stage_affine(u):
             if scalar_makes_inner(u):
                 basis = work3.tile([P, UNIT], BF16, align_bytes=64)
-                nc.scalar.activation(out=basis[:], in_=live[u]["inner"][:], func=ACT.Identity, bias=1.0, scale=1.0)
+                sign = -1.0 if u % G == G - 1 else 1.0
+                nc.scalar.activation(out=basis[:], in_=live[u]["inner"][:], func=ACT.Identity, bias=1.0, scale=sign)
                 live[u]["basis"] = basis
 
         def stage_minimum(u):
@@ -291,7 +270,7 @@ def tile_advancedkanlayer_pa_kernel(tc, x_norm, spline_weight, base_activation, 
 
         def stage_clamp(u):
             cube = live[u]["cube"]
-            factor = {0: -2.0, G - 1: 2.0}.get(u % G, -4.0)
+            factor = 4.0 if u % G == G - 1 else -4.0
             nc.vector.tensor_scalar(out=cube[:], in0=cube[:], scalar1=factor, scalar2=0.0, op0=ALU.mult, op1=ALU.max)
 
         def stage_quantise(u):

@@ -14,15 +14,19 @@ ALU = mybir.AluOpType
 P = 128
 PACK = 4
 B, I, O, G = 2048, 512, 512, 8
-B_TILES = 4
-CHUNK = B_TILES * P
+TILES = 2
+CHUNK = TILES * P
 N_CHUNKS = B // CHUNK
 O_TILES = O // P
+KNOTS = 2
+UNITS = G // KNOTS
 CELL = P * PACK
-UNIT = CHUNK * PACK
-N_UNITS = N_CHUNKS * G
-RING = 8 - B_TILES
+HALF = TILES * CELL
+UNIT = KNOTS * HALF
+N_UNITS = N_CHUNKS * UNITS
+TURNING = 8
 HUGE = 3.0e38
+ROOT6 = math.sqrt(6.0)
 ROOT12 = math.sqrt(12.0)
 
 FLOPS = 2 * B * O * (I * G + I)
@@ -31,12 +35,12 @@ FLOPS = 2 * B * O * (I * G + I)
 def tile_advancedkanlayer_pa_kernel(tc, x_norm, spline_weight, base_activation, grid_points, out):
     nc = tc.nc
     with tc.tile_pool(name="keep", bufs=1) as keep, tc.tile_pool(name="by_chunk", bufs=2) as by_chunk, tc.tile_pool(
-        name="work", bufs=2
-    ) as work, tc.tile_pool(name="work3", bufs=3) as work3, tc.tile_pool(name="work4", bufs=4) as work4, tc.tile_pool(name="tenths", bufs=6) as tenths, tc.psum_pool(
-        name="psum_ring", bufs=RING
-    ) as psum_ring, tc.psum_pool(
-        name="psum_acc", bufs=B_TILES
-    ) as psum_acc:
+        name="turned_x", bufs=4
+    ) as turned_x, tc.tile_pool(name="work", bufs=2) as work, tc.tile_pool(name="work3", bufs=3) as work3, tc.tile_pool(
+        name="queue", bufs=6
+    ) as queue, tc.psum_pool(name="psum_cells", bufs=KNOTS * TILES) as psum_cells, tc.psum_pool(
+        name="psum_side", bufs=2
+    ) as psum_side, tc.psum_pool(name="psum_acc", bufs=TILES) as psum_acc:
         ident = keep.tile([P, P], BF16)
         make_identity(nc, ident[:])
         ident_f32 = keep.tile([P, P], F32)
@@ -44,20 +48,26 @@ def tile_advancedkanlayer_pa_kernel(tc, x_norm, spline_weight, base_activation, 
 
         x_sb = keep.tile([P, B // P, I], BF16)
         x_rows = x_norm.rearrange("(r p) i -> p r i", p=P)
-        nc.sync.dma_start(out=x_sb[:, 0:B_TILES, :], in_=x_rows[:, 0:B_TILES, :])
         grid_bf = keep.tile([P, G], BF16)
-        nc.sync.dma_start(out=grid_bf[:], in_=grid_points.partition_broadcast(P))
         a_sb = keep.tile([P, O_TILES, I], BF16)
-        nc.sync.dma_start(out=a_sb[:], in_=base_activation.rearrange("(s p) i -> p s i", p=P))
         w_sb = keep.tile([P, O_TILES, PACK, P, G], BF16)
+
+        def load_x(first, last):
+            nc.sync.dma_start(out=x_sb[:, first:last, :], in_=x_rows[:, first:last, :])
+
+        load_x(0, TILES)
+        nc.sync.dma_start(out=grid_bf[:], in_=grid_points.partition_broadcast(P))
         for s in range(O_TILES):
             nc.sync.dma_start(
                 out=w_sb[:, s], in_=spline_weight[s * P : (s + 1) * P].rearrange("o (t q) g -> o t q g", t=PACK)
             )
-        for c in range(1, N_CHUNKS):
-            nc.sync.dma_start(
-                out=x_sb[:, c * B_TILES : (c + 1) * B_TILES, :], in_=x_rows[:, c * B_TILES : (c + 1) * B_TILES, :]
-            )
+            if s == 0:
+                load_x(TILES, 2 * TILES)
+        nc.sync.dma_start(out=a_sb[:], in_=base_activation.rearrange("(s p) i -> p s i", p=P))
+        for r in range(2 * TILES, B // P, 4):
+            load_x(r, min(r + 4, B // P))
+
+        column_tiles = []
 
         def of_knots(factor, offset, last_offset):
             columns = keep.tile([P, G], F32, name="columns%d" % len(column_tiles))
@@ -68,8 +78,11 @@ def tile_advancedkanlayer_pa_kernel(tc, x_norm, spline_weight, base_activation, 
                 )
             return columns
 
-        column_tiles = []
-        knot = of_knots(1.0, 0.0, 0.0)
+        knots_and_ones = keep.tile([P, UNITS, KNOTS + 1], F32)
+        nc.vector.memset(knots_and_ones[:], 1.0)
+        nc.vector.tensor_copy(out=knots_and_ones[:, :, 0:KNOTS], in_=grid_bf[:].rearrange("p (q j) -> p q j", j=KNOTS))
+        minus_g = of_knots(-1.0, 0.0, 0.0)
+        minus_root6_g = of_knots(-ROOT6, 0.0, 0.0)
         minus_root12_g = of_knots(-ROOT12, 0.0, 0.0)
         y_offset = of_knots(-1.0, -1.0, 1.0)
         half_y_offset = of_knots(-0.5, -0.5, 0.5)
@@ -80,235 +93,257 @@ def tile_advancedkanlayer_pa_kernel(tc, x_norm, spline_weight, base_activation, 
         w_codes = keep.tile([P, G, O], U32, align_bytes=64)
         w_scales = keep.tile([P, G, O], U8, align_bytes=64)
 
-        def transpose_eight(blocks, grouped):
-            turned = psum_ring.tile([P, len(blocks), PACK, P], BF16, tag="bank")
-            for j in range(len(blocks)):
-                for t in range(PACK):
-                    nc.tensor.transpose(out=turned[:, j, t, :], in_=blocks[j][t], identity=ident[:])
-            nc.scalar.copy(out=grouped, in_=turned[:].rearrange("p j t r -> p j r t"))
+        waiting = []
 
-        def turn_pair(block, s, grouped):
-            transpose_eight(
-                [[block(s + j, t) for t in range(PACK)] for j in range(2)],
-                grouped[:, s * P : (s + 2) * P, :].rearrange("p (j r) t -> p j r t", j=2),
-            )
+        def turn_pair(block, grouped):
+            turned = psum_side.tile([P, 2, PACK, P], BF16, tag="side")
+            for j in range(2):
+                for t in range(PACK):
+                    nc.tensor.transpose(out=turned[:, j, t, :], in_=block(j, t), identity=ident[:])
+            waiting.append((turned, grouped))
+
+        def copy_pair():
+            if waiting:
+                turned, grouped = waiting.pop(0)
+                nc.scalar.copy(
+                    out=grouped.rearrange("p (j r) t -> p j r t", j=2), in_=turned[:].rearrange("p j t r -> p j r t")
+                )
+
+        def quantise(codes, scales, grouped):
+            nc.vector.quantize_mx(out=codes.bitcast(FP8X4), scales=scales, in_=grouped.rearrange("p n t -> p (n t)"))
 
         def turn_base_weights(s):
-            turn_pair(lambda s, t: a_sb[:, s, t * P : (t + 1) * P], s, a_grouped[:])
+            turn_pair(lambda j, t: a_sb[:, s + j, t * P : (t + 1) * P], a_grouped[:, s * P : (s + 2) * P, :])
 
         def quantise_base_weights():
-            nc.vector.quantize_mx(
-                out=a_codes[:].bitcast(FP8X4), scales=a_scales[:], in_=a_grouped[:].rearrange("p o t -> p (o t)")
-            )
+            quantise(a_codes[:], a_scales[:], a_grouped[:])
 
         w_turned = {}
 
         def turn_spline_weights(g, s):
             if s == 0:
                 w_turned[g] = work.tile([P, O, PACK], BF16, align_bytes=64, name="w_grouped")
-            turn_pair(lambda s, t: w_sb[:, s, t, :, g], s, w_turned[g][:])
+            turn_pair(lambda j, t: w_sb[:, s + j, t, :, g], w_turned[g][:, s * P : (s + 2) * P, :])
 
         def quantise_spline_weights(g):
-            nc.vector.quantize_mx(
-                out=w_codes[:, g, :].bitcast(FP8X4),
-                scales=w_scales[:, g, :],
-                in_=w_turned[g][:].rearrange("p o t -> p (o t)"),
-            )
+            quantise(w_codes[:, g, :], w_scales[:, g, :], w_turned[g][:])
 
         x_turned = {}
         x_halved = {}
+        x_quantised = {}
+        base_tenth = {}
 
-        def halve_chunk(c):
-            minus_half_x = by_chunk.tile([P, B_TILES, I], F32)
-            engine = nc.vector if c == 0 else nc.gpsimd
+        def turn_chunk(c):
+            x_turned[c] = turned_x.tile([P, CHUNK, PACK], BF16, align_bytes=64, name="x_grouped")
+            turn_pair(lambda j, t: x_sb[:, c * TILES + j, t * P : (t + 1) * P], x_turned[c][:])
+
+        def halve_chunk(c, engine):
+            x_halved[c] = by_chunk.tile([P, TILES, I], F32, name="minus_half_x")
             engine.tensor_scalar(
-                out=minus_half_x[:],
-                in0=x_sb[:, c * B_TILES : (c + 1) * B_TILES, :],
+                out=x_halved[c][:],
+                in0=x_sb[:, c * TILES : (c + 1) * TILES, :],
                 scalar1=-0.5,
                 scalar2=0.0,
                 op0=ALU.mult,
                 op1=ALU.add,
             )
-            x_halved[c] = minus_half_x
-
-        def turn_chunk(c, s):
-            if s == 0:
-                x_turned[c] = by_chunk.tile([P, CHUNK, PACK], BF16, align_bytes=64, name="x_grouped")
-            turn_pair(lambda s, t: x_sb[:, c * B_TILES + s, t * P : (t + 1) * P], s, x_turned[c][:])
-
-        x_quantised = {}
 
         def quantise_chunk(c):
             x_codes = by_chunk.tile([P, CHUNK], U32, align_bytes=64)
             x_scales = by_chunk.tile([P, CHUNK], U8, align_bytes=64)
-            nc.vector.quantize_mx(
-                out=x_codes[:].bitcast(FP8X4), scales=x_scales[:], in_=x_turned[c][:].rearrange("p b t -> p (b t)")
-            )
+            quantise(x_codes[:], x_scales[:], x_turned[c][:])
             x_quantised[c] = (x_codes, x_scales)
 
-        base_tenth = {}
-
-        def base_product(c, r):
+        def base_product(c):
             x_codes, x_scales = x_quantised[c]
-            rows = slice(r * P, (r + 1) * P)
-            base_ps = psum_ring.tile([P, O], F32, tag="bank")
-            nc.tensor.matmul_mx(
-                out=base_ps[:],
-                lhsT=x_codes[:, rows].bitcast(FP8X4),
-                lhsT_scale=x_scales[:, rows],
-                rhs=a_codes[:].bitcast(FP8X4),
-                rhs_scale=a_scales[:],
-                start=True,
-                stop=True,
-            )
-            tenth = tenths.tile([P, O], F32)
-            nc.scalar.mul(out=tenth[:], in_=base_ps[:], mul=0.1)
-            base_tenth[c * B_TILES + r] = tenth
+            for r in range(TILES):
+                rows = slice(r * P, (r + 1) * P)
+                base_ps = psum_side.tile([P, O], F32, tag="side")
+                nc.tensor.matmul_mx(
+                    out=base_ps[:],
+                    lhsT=x_codes[:, rows].bitcast(FP8X4),
+                    lhsT_scale=x_scales[:, rows],
+                    rhs=a_codes[:].bitcast(FP8X4),
+                    rhs_scale=a_scales[:],
+                    start=True,
+                    stop=True,
+                )
+                tenth = queue.tile([P, O], F32)
+                nc.scalar.mul(out=tenth[:], in_=base_ps[:], mul=0.1)
+                base_tenth[c, r] = tenth
 
         live = {}
         acc = {}
 
-        def x_of(u):
-            return x_turned[u // G][:].rearrange("p b t -> p (b t)")
+        def place(u):
+            c, q = divmod(u, UNITS)
+            return c, range(q * KNOTS, (q + 1) * KNOTS)
 
-        def scalar_makes_inner(u):
-            return u >= G or u % G == G - 1
+        def by_max(u, g):
+            return u < TURNING or g in (0, G - 1)
 
-        def stage_max(u):
-            c, g = divmod(u, G)
-            knot_now = work.tile([P, 1], F32)
-            nc.vector.tensor_copy(out=knot_now[:], in_=knot[:, g : g + 1])
-            larger = work.tile([P, B_TILES, I], F32)
-            last = g == G - 1
-            nc.gpsimd.tensor_scalar(
-                out=larger[:],
-                in0=x_sb[:, c * B_TILES : (c + 1) * B_TILES, :],
-                scalar1=knot_now[:] if last else HUGE,
-                scalar2=-HUGE if last else knot_now[:],
-                op0=ALU.min,
-                op1=ALU.max,
-            )
-            live[u] = {"larger": larger}
+        def half(tile, j):
+            return tile[:, j * HALF : (j + 1) * HALF]
 
-        def stage_square(u):
-            g = u % G
-            inner = work4.tile([P, UNIT], F32)
-            nc.scalar.activation(
-                out=inner[:], in_=x_of(u), func=ACT.Square, bias=minus_root12_g[:, g : g + 1], scale=ROOT12
-            )
-            live[u]["inner"] = inner
+        def cell(tile, j, r):
+            start = j * HALF + r * CELL
+            return tile[:, start : start + CELL].rearrange("p (b t) -> p b t", t=PACK)
 
-        def turn_cell(u, r):
-            z = psum_ring.tile([P, PACK, P], F32, tag="bank")
-            for t in range(PACK):
-                features = slice(t * P, (t + 1) * P)
-                for source, first in ((live[u]["larger"], True), (x_halved[u // G], False)):
-                    nc.tensor.matmul(
-                        out=z[:, t, :],
-                        lhsT=source[:, r, features],
-                        rhs=ident_f32[:],
-                        is_transpose=True,
-                        start=first,
-                        stop=not first,
+        def hand_out(u):
+            columns = work.tile([P, KNOTS + 1], F32)
+            nc.vector.tensor_copy(out=columns[:], in_=knots_and_ones[:, u % UNITS, :])
+            return columns
+
+        def stage_rows(u, columns):
+            c, knots = place(u)
+            x_here = x_sb[:, c * TILES : (c + 1) * TILES, :]
+            rows = work3.tile([P, KNOTS, TILES, I], F32)
+            for j, g in enumerate(knots):
+                if not by_max(u, g):
+                    nc.scalar.activation(out=rows[:, j], in_=x_here, func=ACT.Abs, bias=minus_g[:, g : g + 1], scale=1.0)
+                elif g == G - 1:
+                    nc.gpsimd.tensor_scalar(
+                        out=rows[:, j], in0=x_here, scalar1=columns[:, j : j + 1], scalar2=-HUGE, op0=ALU.min, op1=ALU.max
                     )
-            live[u][r] = z[:].rearrange("p t b -> p b t")
+                else:
+                    nc.gpsimd.tensor_scalar(
+                        out=rows[:, j], in0=x_here, scalar1=HUGE, scalar2=columns[:, j : j + 1], op0=ALU.min, op1=ALU.max
+                    )
+            live[u] = {"rows": rows}
 
         def stage_turn(u):
-            for r in range(B_TILES):
-                turn_cell(u, r)
+            c, knots = place(u)
+            live[u]["z"] = {}
+            for j, g in enumerate(knots):
+                sources = [live[u]["rows"][:, j]] + ([x_halved[c][:]] if by_max(u, g) else [])
+                for r in range(TILES):
+                    z = psum_cells.tile([P, PACK, P], F32)
+                    for t in range(PACK):
+                        for source in sources:
+                            nc.tensor.matmul(
+                                out=z[:, t, :],
+                                lhsT=source[:, r, t * P : (t + 1) * P],
+                                rhs=ident_f32[:],
+                                is_transpose=True,
+                                start=source is sources[0],
+                                stop=source is sources[-1],
+                            )
+                    live[u]["z"][j, r] = z[:].rearrange("p t b -> p b t")
+
+        def stage_squares(u):
+            c, knots = place(u)
+            inner = work3.tile([P, UNIT], F32)
+            outer = work.tile([P, UNIT], F32)
+            x_here = x_turned[c][:].rearrange("p b t -> p (b t)")
+
+            def outer_square(j, g, r):
+                bias, scale = (y_offset[:, g : g + 1], 2.0) if by_max(u, g) else (1.0, -1.0)
+                nc.scalar.activation(
+                    out=cell(outer, j, r), in_=live[u]["z"][j, r], func=ACT.Square, bias=bias, scale=scale
+                )
+
+            def inner_square(j, g):
+                root, bias = (ROOT12, minus_root12_g) if by_max(u, g) else (ROOT6, minus_root6_g)
+                nc.scalar.activation(
+                    out=half(inner, j), in_=x_here, func=ACT.Square, bias=bias[:, g : g + 1], scale=root
+                )
+
+            outer_square(0, knots[0], 0)
+            inner_square(0, knots[0])
+            outer_square(0, knots[0], 1)
+            inner_square(1, knots[1])
+            outer_square(1, knots[1], 0)
+            outer_square(1, knots[1], 1)
+            live[u]["inner"] = inner
+            live[u]["outer"] = outer
 
         def stage_products(u):
-            g = u % G
-            inner = live[u]["inner"]
-            cube = work3.tile([P, UNIT], BF16, align_bytes=64)
-            outer = work.tile([P, UNIT], F32)
-
-            def product(r, factor, result):
-                cell = slice(r * CELL, (r + 1) * CELL)
-                nc.vector.scalar_tensor_tensor(
-                    out=result[:, cell].rearrange("p (b t) -> p b t", t=PACK),
-                    in0=live[u][r],
-                    scalar=half_y_offset[:, g : g + 1],
-                    in1=factor[:, cell].rearrange("p (b t) -> p b t", t=PACK),
-                    op0=ALU.add,
-                    op1=ALU.mult,
-                )
-
-            for r in range(B_TILES):
-                nc.scalar.activation(
-                    out=outer[:, r * CELL : (r + 1) * CELL].rearrange("p (b t) -> p b t", t=PACK),
-                    in_=live[u][r],
-                    func=ACT.Square,
-                    bias=y_offset[:, g : g + 1],
-                    scale=2.0,
-                )
-            for r in range(B_TILES + 1):
-                if r < B_TILES:
-                    product(r, inner, inner)
-                if r > 0:
-                    product(r - 1, outer, cube)
+            inner, outer = live[u]["inner"], live[u]["outer"]
+            cube = work.tile([P, UNIT], BF16, align_bytes=64)
+            for j, g in enumerate(place(u)[1]):
+                for r in range(TILES):
+                    for factor, result in ((inner, inner), (outer, cube)):
+                        nc.vector.scalar_tensor_tensor(
+                            out=cell(result, j, r),
+                            in0=live[u]["z"][j, r],
+                            scalar=half_y_offset[:, g : g + 1] if by_max(u, g) else -1.0,
+                            in1=cell(factor, j, r),
+                            op0=ALU.add,
+                            op1=ALU.mult,
+                        )
             live[u]["cube"] = cube
 
-        def stage_affine(u):
-            if scalar_makes_inner(u):
-                basis = work3.tile([P, UNIT], BF16, align_bytes=64)
-                sign = -1.0 if u % G == G - 1 else 1.0
-                nc.scalar.activation(out=basis[:], in_=live[u]["inner"][:], func=ACT.Identity, bias=1.0, scale=sign)
-                live[u]["basis"] = basis
+        def grouped_knots(u, value):
+            values = [value(g) for g in place(u)[1]]
+            if values[0] == values[1]:
+                return [(0, UNIT, values[0])]
+            return [(0, HALF, values[0]), (HALF, UNIT, values[1])]
 
-        def stage_minimum(u):
-            cube = live[u]["cube"]
-            if scalar_makes_inner(u):
-                basis = live[u]["basis"]
-                nc.vector.tensor_tensor(out=basis[:], in0=basis[:], in1=cube[:], op=ALU.min)
-            else:
-                basis = work3.tile([P, UNIT], BF16, align_bytes=64)
-                nc.vector.scalar_tensor_tensor(
-                    out=basis[:], in0=live[u]["inner"][:], scalar=1.0, in1=cube[:], op0=ALU.add, op1=ALU.min
+        def stage_affine(u, columns):
+            basis = work3.tile([P, UNIT], BF16, align_bytes=64)
+            one = columns[:, KNOTS : KNOTS + 1]
+            for first, last, sign in grouped_knots(u, lambda g: -1.0 if g == G - 1 else 1.0):
+                nc.gpsimd.tensor_scalar(
+                    out=basis[:, first:last],
+                    in0=live[u]["inner"][:, first:last],
+                    scalar1=sign,
+                    scalar2=one,
+                    op0=ALU.mult,
+                    op1=ALU.add,
                 )
-            live[u] = {"basis": basis}
+            live[u]["basis"] = basis
 
         def stage_clamp(u):
             cube = live[u]["cube"]
-            factor = 4.0 if u % G == G - 1 else -4.0
-            nc.vector.tensor_scalar(out=cube[:], in0=cube[:], scalar1=factor, scalar2=0.0, op0=ALU.mult, op1=ALU.max)
-
-        def stage_quantise(u):
-            basis = live[u]["basis"]
-            n_codes = work3.tile([P, CHUNK], U32, align_bytes=64)
-            n_scales = work3.tile([P, CHUNK], U8, align_bytes=64)
-            nc.vector.quantize_mx(out=n_codes[:].bitcast(FP8X4), scales=n_scales[:], in_=basis[:])
-            live[u] = {"codes": n_codes, "scales": n_scales}
-
-        def stage_matmul(u):
-            c, g = divmod(u, G)
-            n_codes, n_scales = live[u]["codes"], live[u]["scales"]
-            for r in range(B_TILES):
-                if g == 0:
-                    acc[r] = psum_acc.tile([P, O], F32, name="acc")
-                rows = slice(r * P, (r + 1) * P)
-                nc.tensor.matmul_mx(
-                    out=acc[r][:],
-                    lhsT=n_codes[:, rows].bitcast(FP8X4),
-                    lhsT_scale=n_scales[:, rows],
-                    rhs=w_codes[:, g, :].bitcast(FP8X4),
-                    rhs_scale=w_scales[:, g, :],
-                    start=(g == 0),
-                    stop=(g == G - 1),
+            for first, last, factor in grouped_knots(
+                u, lambda g: 4.0 if g == G - 1 else -4.0 if by_max(u, g) else -2.0
+            ):
+                nc.vector.tensor_scalar(
+                    out=cube[:, first:last],
+                    in0=cube[:, first:last],
+                    scalar1=factor,
+                    scalar2=0.0,
+                    op0=ALU.mult,
+                    op1=ALU.max,
                 )
 
-        def stage_store(u):
-            c, g = divmod(u, G)
-            if g == G - 1:
-                for r in range(B_TILES):
-                    total = work.tile([P, O], F32)
-                    nc.vector.tensor_tensor(out=total[:], in0=acc[r][:], in1=base_tenth[c * B_TILES + r][:], op=ALU.add)
-                    first = c * CHUNK + r * P
-                    nc.sync.dma_start(out=out[first : first + P, :], in_=total[:])
+        def stage_minimum(u):
+            basis = live[u]["basis"]
+            nc.vector.tensor_tensor(out=basis[:], in0=basis[:], in1=live[u]["cube"][:], op=ALU.min)
 
-        def run(stage, u):
+        def stage_quantise(u):
+            codes = queue.tile([P, KNOTS * CHUNK], U32, align_bytes=64)
+            scales = queue.tile([P, KNOTS * CHUNK], U8, align_bytes=64)
+            nc.vector.quantize_mx(out=codes[:].bitcast(FP8X4), scales=scales[:], in_=live[u]["basis"][:])
+            live[u] = {"codes": codes, "scales": scales}
+
+        def stage_matmul(u):
+            codes, scales = live[u]["codes"], live[u]["scales"]
+            for j, g in enumerate(place(u)[1]):
+                for r in range(TILES):
+                    if g == 0:
+                        acc[r] = psum_acc.tile([P, O], F32, name="acc")
+                    rows = slice(j * CHUNK + r * P, j * CHUNK + (r + 1) * P)
+                    nc.tensor.matmul_mx(
+                        out=acc[r][:],
+                        lhsT=codes[:, rows].bitcast(FP8X4),
+                        lhsT_scale=scales[:, rows],
+                        rhs=w_codes[:, g, :].bitcast(FP8X4),
+                        rhs_scale=w_scales[:, g, :],
+                        start=(g == 0),
+                        stop=(g == G - 1),
+                    )
+
+        def store_chunk(c):
+            for r in range(TILES):
+                total = work.tile([P, O], F32)
+                nc.vector.tensor_tensor(out=total[:], in0=acc[r][:], in1=base_tenth[c, r][:], op=ALU.add)
+                first = c * CHUNK + r * P
+                nc.sync.dma_start(out=out[first : first + P, :], in_=total[:])
+
+        def run(stage, u, *others):
             if 0 <= u < N_UNITS:
-                stage(u)
+                stage(u, *others)
 
         with tc.manual_schedule(
             engines={
@@ -318,40 +353,58 @@ def tile_advancedkanlayer_pa_kernel(tc, x_norm, spline_weight, base_activation, 
                 mybir.EngineType.Pool,
             }
         ):
-            halve_chunk(0)
-            stage_max(0)
-            turn_chunk(0, 0)
-            turn_chunk(0, 2)
+            columns = hand_out(0)
+            stage_rows(0, columns)
+            halve_chunk(0, nc.vector)
+            columns = hand_out(1)
+            stage_rows(1, columns)
+            turn_chunk(0)
+            copy_pair()
             stage_turn(0)
-            stage_square(0)
+            stage_squares(0)
+            multiplied = 0
+            stored = 0
+            base_done = 0
             for k in range(N_UNITS + 3):
-                c, step = divmod(k, G)
-                run(stage_max, k + 1)
+                c, q = divmod(k, UNITS)
+                columns = hand_out(k + 2)
+                run(stage_affine, k - 1, columns)
+                if k + 2 < N_UNITS:
+                    if q == 0 and c + 1 < N_CHUNKS:
+                        halve_chunk(c + 1, nc.gpsimd)
                 run(stage_products, k)
-                run(stage_store, k - 3)
-                run(stage_square, k + 1)
-                if c == 0:
+                if k < TURNING:
                     turn_spline_weights(k, 0)
                     turn_spline_weights(k, 2)
-                elif step in (4, 5) and c + 1 < N_CHUNKS:
-                    turn_chunk(c + 1, 2 * (step - 4))
-                if k in (1, 2):
-                    turn_base_weights(2 * (k - 1))
-                if c == 0 and step in (5, 6):
-                    turn_chunk(1, 2 * (step - 5))
-                if 4 <= step and c < N_CHUNKS:
-                    base_product(c, step - 4)
-                if c + 1 < N_CHUNKS and step == 4:
-                    halve_chunk(c + 1)
+                elif q == 1 and c + 1 < N_CHUNKS:
+                    turn_chunk(c + 1)
                 run(stage_turn, k + 1)
-                run(stage_affine, k - 1)
-                run(stage_minimum, k - 2)
+                run(stage_squares, k + 1)
+                copy_pair()
+                run(stage_rows, k + 2, columns)
+                copy_pair()
+                if k in (1, 3, 5, 7):
+                    if k % 4 == 1:
+                        turn_chunk(k // 4 + 1)
+                    else:
+                        turn_base_weights(k // 4 * 2)
+                    copy_pair()
+                run(stage_minimum, k - 1)
                 run(stage_clamp, k)
-                if 1 <= k <= G:
+                if 1 <= k <= TURNING:
                     quantise_spline_weights(k - 1)
-                if k == 3:
+                if k == TURNING:
                     quantise_base_weights()
-                if step == 3 and c < N_CHUNKS:
-                    quantise_chunk(c)
-                run(stage_quantise, k - 2)
-                run(stage_matmul, k - 2)
+                if k >= TURNING and base_done < N_CHUNKS and base_done <= c:
+                    quantise_chunk(base_done)
+                    base_product(base_done)
+                    base_done += 1
+                if multiplied == (stored + 1) * UNITS:
+                    store_chunk(stored)
+                    stored += 1
+                run(stage_quantise, k - 1)
+                for u in range(multiplied, min(multiplied + 2, N_UNITS)):
+                    ready = u <= k - 1 and k >= min(KNOTS * (u + 1), TURNING) and u // UNITS == stored
+                    if u == multiplied and ready:
+                        stage_matmul(u)
+                        multiplied += 1

@@ -172,6 +172,10 @@ def tile_advancedkanlayer_pa_kernel(tc, x_norm, spline_weight, base_activation, 
                 nc.scalar.mul(out=tenth[:], in_=base_ps[:], mul=0.1)
                 base_tenth[c, r] = tenth
 
+        def keep_clock():
+            unread = psum_side.tile([P, P], F32, tag="side")
+            nc.tensor.matmul(out=unread[:], lhsT=ident_f32[:], rhs=ident_f32[:], start=True, stop=True)
+
         live = {}
         acc = {}
 
@@ -180,7 +184,7 @@ def tile_advancedkanlayer_pa_kernel(tc, x_norm, spline_weight, base_activation, 
             return c, range(q * KNOTS, (q + 1) * KNOTS)
 
         def by_max(u, g):
-            return u < TURNING or g in (0, G - 1)
+            return g in (0, G - 1) or (u < TURNING and g % KNOTS == 0)
 
         def half(tile, j):
             return tile[:, j * HALF : (j + 1) * HALF]
@@ -196,17 +200,18 @@ def tile_advancedkanlayer_pa_kernel(tc, x_norm, spline_weight, base_activation, 
 
         def stage_rows(u, columns):
             c, knots = place(u)
+            engine = nc.vector if u == 0 else nc.gpsimd
             x_here = x_sb[:, c * TILES : (c + 1) * TILES, :]
             rows = work3.tile([P, KNOTS, TILES, I], F32)
             for j, g in enumerate(knots):
                 if not by_max(u, g):
                     nc.scalar.activation(out=rows[:, j], in_=x_here, func=ACT.Abs, bias=minus_g[:, g : g + 1], scale=1.0)
                 elif g == G - 1:
-                    nc.gpsimd.tensor_scalar(
+                    engine.tensor_scalar(
                         out=rows[:, j], in0=x_here, scalar1=columns[:, j : j + 1], scalar2=-HUGE, op0=ALU.min, op1=ALU.max
                     )
                 else:
-                    nc.gpsimd.tensor_scalar(
+                    engine.tensor_scalar(
                         out=rows[:, j], in0=x_here, scalar1=HUGE, scalar2=columns[:, j : j + 1], op0=ALU.min, op1=ALU.max
                     )
             live[u] = {"rows": rows}
@@ -229,6 +234,7 @@ def tile_advancedkanlayer_pa_kernel(tc, x_norm, spline_weight, base_activation, 
                                 stop=source is sources[-1],
                             )
                     live[u]["z"][j, r] = z[:].rearrange("p t b -> p b t")
+                    keep_clock()
 
         def stage_squares(u):
             c, knots = place(u)
@@ -283,14 +289,13 @@ def tile_advancedkanlayer_pa_kernel(tc, x_norm, spline_weight, base_activation, 
             basis = work3.tile([P, UNIT], BF16, align_bytes=64)
             one = columns[:, KNOTS : KNOTS + 1]
             for first, last, sign in grouped_knots(u, lambda g: -1.0 if g == G - 1 else 1.0):
-                nc.gpsimd.tensor_scalar(
-                    out=basis[:, first:last],
-                    in0=live[u]["inner"][:, first:last],
-                    scalar1=sign,
-                    scalar2=one,
-                    op0=ALU.mult,
-                    op1=ALU.add,
-                )
+                inner = live[u]["inner"][:, first:last]
+                if u == N_UNITS - 1:
+                    nc.scalar.activation(out=basis[:, first:last], in_=inner, func=ACT.Identity, bias=1.0, scale=sign)
+                else:
+                    nc.gpsimd.tensor_scalar(
+                        out=basis[:, first:last], in0=inner, scalar1=sign, scalar2=one, op0=ALU.mult, op1=ALU.add
+                    )
             live[u]["basis"] = basis
 
         def stage_clamp(u):
@@ -317,9 +322,9 @@ def tile_advancedkanlayer_pa_kernel(tc, x_norm, spline_weight, base_activation, 
             nc.vector.quantize_mx(out=codes[:].bitcast(FP8X4), scales=scales[:], in_=live[u]["basis"][:])
             live[u] = {"codes": codes, "scales": scales}
 
-        def stage_matmul(u):
+        def stage_matmul(u, j):
             codes, scales = live[u]["codes"], live[u]["scales"]
-            for j, g in enumerate(place(u)[1]):
+            for g in place(u)[1][j : j + 1]:
                 for r in range(TILES):
                     if g == 0:
                         acc[r] = psum_acc.tile([P, O], F32, name="acc")
@@ -353,8 +358,7 @@ def tile_advancedkanlayer_pa_kernel(tc, x_norm, spline_weight, base_activation, 
                 mybir.EngineType.Pool,
             }
         ):
-            columns = hand_out(0)
-            stage_rows(0, columns)
+            stage_rows(0, knots_and_ones[:, 0, :])
             halve_chunk(0, nc.vector)
             columns = hand_out(1)
             stage_rows(1, columns)
@@ -362,49 +366,53 @@ def tile_advancedkanlayer_pa_kernel(tc, x_norm, spline_weight, base_activation, 
             copy_pair()
             stage_turn(0)
             stage_squares(0)
-            multiplied = 0
-            stored = 0
-            base_done = 0
+            progress = {"multiplied": 0, "stored": 0, "based": 0}
+
+            def multiply(quantised, weighed, most):
+                for n in range(most):
+                    c, g = divmod(progress["multiplied"], G)
+                    u = progress["multiplied"] // KNOTS
+                    if u < min(quantised, N_UNITS) and (c > 0 or g < weighed) and c == progress["stored"]:
+                        stage_matmul(u, g % KNOTS)
+                        progress["multiplied"] += 1
+
             for k in range(N_UNITS + 3):
                 c, q = divmod(k, UNITS)
                 columns = hand_out(k + 2)
                 run(stage_affine, k - 1, columns)
-                if k + 2 < N_UNITS:
-                    if q == 0 and c + 1 < N_CHUNKS:
-                        halve_chunk(c + 1, nc.gpsimd)
+                if q == 0 and c + 1 < N_CHUNKS:
+                    halve_chunk(c + 1, nc.gpsimd)
                 run(stage_products, k)
+                copy_pair()
+                run(stage_turn, k + 1)
+                multiply(k - 1, k - 1, KNOTS)
                 if k < TURNING:
                     turn_spline_weights(k, 0)
                     turn_spline_weights(k, 2)
                 elif q == 1 and c + 1 < N_CHUNKS:
                     turn_chunk(c + 1)
-                run(stage_turn, k + 1)
                 run(stage_squares, k + 1)
-                copy_pair()
                 run(stage_rows, k + 2, columns)
                 copy_pair()
-                if k in (1, 3, 5, 7):
-                    if k % 4 == 1:
-                        turn_chunk(k // 4 + 1)
-                    else:
-                        turn_base_weights(k // 4 * 2)
-                    copy_pair()
+                copy_pair()
                 run(stage_minimum, k - 1)
                 run(stage_clamp, k)
                 if 1 <= k <= TURNING:
                     quantise_spline_weights(k - 1)
                 if k == TURNING:
                     quantise_base_weights()
-                if k >= TURNING and base_done < N_CHUNKS and base_done <= c:
-                    quantise_chunk(base_done)
-                    base_product(base_done)
-                    base_done += 1
-                if multiplied == (stored + 1) * UNITS:
-                    store_chunk(stored)
-                    stored += 1
+                if k >= TURNING and progress["based"] < min(c + 1, N_CHUNKS):
+                    quantise_chunk(progress["based"])
+                    base_product(progress["based"])
+                    progress["based"] += 1
+                if progress["multiplied"] == (progress["stored"] + 1) * G:
+                    store_chunk(progress["stored"])
+                    progress["stored"] += 1
                 run(stage_quantise, k - 1)
-                for u in range(multiplied, min(multiplied + 2, N_UNITS)):
-                    ready = u <= k - 1 and k >= min(KNOTS * (u + 1), TURNING) and u // UNITS == stored
-                    if u == multiplied and ready:
-                        stage_matmul(u)
-                        multiplied += 1
+                multiply(k, k, 1)
+                if k in (1, 5):
+                    turn_chunk(k // 4 + 1)
+                if k in (3, 7):
+                    turn_base_weights(k // 4 * 2)
+            if progress["stored"] < N_CHUNKS:
+                store_chunk(progress["stored"])

@@ -25,8 +25,8 @@ HALF = TILES * CELL
 UNIT = KNOTS * HALF
 N_UNITS = N_CHUNKS * UNITS
 TURNING = 8
+SHARING = 3
 HUGE = 3.0e38
-ROOT6 = math.sqrt(6.0)
 ROOT12 = math.sqrt(12.0)
 
 FLOPS = 2 * B * O * (I * G + I)
@@ -38,7 +38,9 @@ def tile_advancedkanlayer_pa_kernel(tc, x_norm, spline_weight, base_activation, 
         name="turned_x", bufs=4
     ) as turned_x, tc.tile_pool(name="work", bufs=2) as work, tc.tile_pool(name="work3", bufs=3) as work3, tc.tile_pool(
         name="queue", bufs=6
-    ) as queue, tc.psum_pool(name="psum_cells", bufs=KNOTS * TILES) as psum_cells, tc.psum_pool(
+    ) as queue, tc.tile_pool(name="work4", bufs=4) as work4, tc.tile_pool(
+        name="halves", bufs=5
+    ) as halves, tc.psum_pool(name="psum_cells", bufs=KNOTS * TILES) as psum_cells, tc.psum_pool(
         name="psum_side", bufs=2
     ) as psum_side, tc.psum_pool(name="psum_acc", bufs=TILES) as psum_acc:
         ident = keep.tile([P, P], BF16)
@@ -69,23 +71,42 @@ def tile_advancedkanlayer_pa_kernel(tc, x_norm, spline_weight, base_activation, 
 
         column_tiles = []
 
-        def of_knots(factor, offset, last_offset):
+        def of_knots(factor, added):
             columns = keep.tile([P, G], F32, name="columns%d" % len(column_tiles))
             column_tiles.append(columns)
-            for knots, added in ((slice(0, G - 1), offset), (slice(G - 1, G), last_offset)):
-                nc.vector.tensor_scalar(
-                    out=columns[:, knots], in0=grid_bf[:, knots], scalar1=factor, scalar2=added, op0=ALU.mult, op1=ALU.add
-                )
+            nc.vector.tensor_scalar(
+                out=columns[:], in0=grid_bf[:], scalar1=factor, scalar2=added, op0=ALU.mult, op1=ALU.add
+            )
             return columns
 
         knots_and_ones = keep.tile([P, UNITS, KNOTS + 1], F32)
-        nc.vector.memset(knots_and_ones[:], 1.0)
+        nc.vector.memset(knots_and_ones[:], -1.0)
         nc.vector.tensor_copy(out=knots_and_ones[:, :, 0:KNOTS], in_=grid_bf[:].rearrange("p (q j) -> p q j", j=KNOTS))
-        minus_g = of_knots(-1.0, 0.0, 0.0)
-        minus_root6_g = of_knots(-ROOT6, 0.0, 0.0)
-        minus_root12_g = of_knots(-ROOT12, 0.0, 0.0)
-        y_offset = of_knots(-1.0, -1.0, 1.0)
-        half_y_offset = of_knots(-0.5, -0.5, 0.5)
+        nc.vector.tensor_scalar(
+            out=knots_and_ones[:, UNITS - 1, KNOTS - 1 : KNOTS],
+            in0=grid_bf[:, G - 1 : G],
+            scalar1=-1.0,
+            scalar2=None,
+            op0=ALU.mult,
+        )
+        minus_half_g = of_knots(-0.5, 0.0)
+        minus_root12_g = of_knots(-ROOT12, 0.0)
+        offset = of_knots(-0.5, -0.5)
+        nc.vector.tensor_scalar(
+            out=offset[:, G - 1 : G], in0=grid_bf[:, G - 1 : G], scalar1=0.5, scalar2=-0.5, op0=ALU.mult, op1=ALU.add
+        )
+        minus_half = keep.tile([P, P], F32)
+        nc.vector.memset(minus_half[:], -0.5)
+        half_step = keep.tile([P, P], F32)
+        nc.vector.memset(half_step[:], 0.0)
+        nc.vector.tensor_scalar(
+            out=half_step[:],
+            in0=half_step[:],
+            scalar1=offset[:, SHARING : SHARING + 1],
+            scalar2=offset[:, 0:1],
+            op0=ALU.add,
+            op1=ALU.subtract,
+        )
 
         a_grouped = keep.tile([P, O, PACK], BF16, align_bytes=64)
         a_codes = keep.tile([P, O], U32, align_bytes=64)
@@ -130,6 +151,7 @@ def tile_advancedkanlayer_pa_kernel(tc, x_norm, spline_weight, base_activation, 
 
         x_turned = {}
         x_halved = {}
+        x_negated = {}
         x_quantised = {}
         base_tenth = {}
 
@@ -137,15 +159,25 @@ def tile_advancedkanlayer_pa_kernel(tc, x_norm, spline_weight, base_activation, 
             x_turned[c] = turned_x.tile([P, CHUNK, PACK], BF16, align_bytes=64, name="x_grouped")
             turn_pair(lambda j, t: x_sb[:, c * TILES + j, t * P : (t + 1) * P], x_turned[c][:])
 
-        def halve_chunk(c, engine):
-            x_halved[c] = by_chunk.tile([P, TILES, I], F32, name="minus_half_x")
+        def halve_chunk(c, g, engine):
+            x_halved[c, g] = halves.tile([P, TILES, I], F32, name="half_x")
             engine.tensor_scalar(
-                out=x_halved[c][:],
+                out=x_halved[c, g][:],
                 in0=x_sb[:, c * TILES : (c + 1) * TILES, :],
-                scalar1=-0.5,
-                scalar2=0.0,
+                scalar1=0.5 if g == G - 1 else -0.5,
+                scalar2=offset[:, g : g + 1],
                 op0=ALU.mult,
                 op1=ALU.add,
+            )
+
+        def negate_chunk(c):
+            x_negated[c] = by_chunk.tile([P, TILES, I], BF16, name="minus_x")
+            nc.vector.tensor_scalar(
+                out=x_negated[c][:],
+                in0=x_sb[:, c * TILES : (c + 1) * TILES, :],
+                scalar1=-1.0,
+                scalar2=None,
+                op0=ALU.mult,
             )
 
         def quantise_chunk(c):
@@ -168,7 +200,7 @@ def tile_advancedkanlayer_pa_kernel(tc, x_norm, spline_weight, base_activation, 
                     start=True,
                     stop=True,
                 )
-                tenth = queue.tile([P, O], F32)
+                tenth = work4.tile([P, O], F32)
                 nc.scalar.mul(out=tenth[:], in_=base_ps[:], mul=0.1)
                 base_tenth[c, r] = tenth
 
@@ -184,7 +216,17 @@ def tile_advancedkanlayer_pa_kernel(tc, x_norm, spline_weight, base_activation, 
             return c, range(q * KNOTS, (q + 1) * KNOTS)
 
         def by_max(u, g):
-            return g in (0, G - 1) or (u < TURNING and g % KNOTS == 0)
+            return g in (0, G - 1) or (g % KNOTS == 0 if u < TURNING else g == SHARING)
+
+        def addends(u, g):
+            c, knots = place(u)
+            rows = live[u]["rows"]
+            parts = [lambda r, features: rows[:, g - knots[0], r, features]]
+            if not by_max(u, g):
+                return parts + [lambda r, features: minus_half[:]]
+            if (c, g) in x_halved:
+                return parts + [lambda r, features: x_halved[c, g][:, r, features]]
+            return parts + [lambda r, features: x_halved[c, 0][:, r, features], lambda r, features: half_step[:]]
 
         def half(tile, j):
             return tile[:, j * HALF : (j + 1) * HALF]
@@ -204,34 +246,43 @@ def tile_advancedkanlayer_pa_kernel(tc, x_norm, spline_weight, base_activation, 
             x_here = x_sb[:, c * TILES : (c + 1) * TILES, :]
             rows = work3.tile([P, KNOTS, TILES, I], F32)
             for j, g in enumerate(knots):
-                if not by_max(u, g):
-                    nc.scalar.activation(out=rows[:, j], in_=x_here, func=ACT.Abs, bias=minus_g[:, g : g + 1], scale=1.0)
-                elif g == G - 1:
+                if by_max(u, g):
                     engine.tensor_scalar(
-                        out=rows[:, j], in0=x_here, scalar1=columns[:, j : j + 1], scalar2=-HUGE, op0=ALU.min, op1=ALU.max
+                        out=rows[:, j],
+                        in0=x_negated[c][:] if g == G - 1 else x_here,
+                        scalar1=HUGE,
+                        scalar2=columns[:, j : j + 1],
+                        op0=ALU.min,
+                        op1=ALU.max,
                     )
                 else:
-                    engine.tensor_scalar(
-                        out=rows[:, j], in0=x_here, scalar1=HUGE, scalar2=columns[:, j : j + 1], op0=ALU.min, op1=ALU.max
+                    nc.scalar.activation(
+                        out=rows[:, j], in_=x_here, func=ACT.Abs, bias=minus_half_g[:, g : g + 1], scale=0.5
                     )
             live[u] = {"rows": rows}
+
+        def stage_halves(u):
+            c, knots = place(u)
+            for g in knots:
+                if by_max(u, g):
+                    halve_chunk(c, g, nc.vector)
 
         def stage_turn(u):
             c, knots = place(u)
             live[u]["z"] = {}
             for j, g in enumerate(knots):
-                sources = [live[u]["rows"][:, j]] + ([x_halved[c][:]] if by_max(u, g) else [])
+                parts = addends(u, g)
                 for r in range(TILES):
                     z = psum_cells.tile([P, PACK, P], F32)
                     for t in range(PACK):
-                        for source in sources:
+                        for i, part in enumerate(parts):
                             nc.tensor.matmul(
                                 out=z[:, t, :],
-                                lhsT=source[:, r, t * P : (t + 1) * P],
+                                lhsT=part(r, slice(t * P, (t + 1) * P)),
                                 rhs=ident_f32[:],
                                 is_transpose=True,
-                                start=source is sources[0],
-                                stop=source is sources[-1],
+                                start=i == 0,
+                                stop=i + 1 == len(parts),
                             )
                     live[u]["z"][j, r] = z[:].rearrange("p t b -> p b t")
                     keep_clock()
@@ -242,84 +293,77 @@ def tile_advancedkanlayer_pa_kernel(tc, x_norm, spline_weight, base_activation, 
             outer = work.tile([P, UNIT], F32)
             x_here = x_turned[c][:].rearrange("p b t -> p (b t)")
 
-            def outer_square(j, g, r):
-                bias, scale = (y_offset[:, g : g + 1], 2.0) if by_max(u, g) else (1.0, -1.0)
+            def outer_square(j, r):
+                nc.scalar.activation(out=cell(outer, j, r), in_=live[u]["z"][j, r], func=ACT.Square, scale=4.0)
+
+            def inner_square(j):
+                g = knots[j]
                 nc.scalar.activation(
-                    out=cell(outer, j, r), in_=live[u]["z"][j, r], func=ACT.Square, bias=bias, scale=scale
+                    out=half(inner, j), in_=x_here, func=ACT.Square, bias=minus_root12_g[:, g : g + 1], scale=ROOT12
                 )
 
-            def inner_square(j, g):
-                root, bias = (ROOT12, minus_root12_g) if by_max(u, g) else (ROOT6, minus_root6_g)
-                nc.scalar.activation(
-                    out=half(inner, j), in_=x_here, func=ACT.Square, bias=bias[:, g : g + 1], scale=root
-                )
-
-            outer_square(0, knots[0], 0)
-            inner_square(0, knots[0])
-            outer_square(0, knots[0], 1)
-            inner_square(1, knots[1])
-            outer_square(1, knots[1], 0)
-            outer_square(1, knots[1], 1)
+            if u == 0:
+                inner_square(0)
+            outer_square(0, 0)
+            if u > 0:
+                inner_square(0)
+            outer_square(0, 1)
+            inner_square(1)
+            outer_square(1, 0)
+            outer_square(1, 1)
             live[u]["inner"] = inner
             live[u]["outer"] = outer
 
         def stage_products(u):
             inner, outer = live[u]["inner"], live[u]["outer"]
             cube = work.tile([P, UNIT], BF16, align_bytes=64)
-            for j, g in enumerate(place(u)[1]):
+            for j in range(KNOTS):
                 for r in range(TILES):
-                    for factor, result in ((inner, inner), (outer, cube)):
-                        nc.vector.scalar_tensor_tensor(
-                            out=cell(result, j, r),
-                            in0=live[u]["z"][j, r],
-                            scalar=half_y_offset[:, g : g + 1] if by_max(u, g) else -1.0,
-                            in1=cell(factor, j, r),
-                            op0=ALU.add,
-                            op1=ALU.mult,
-                        )
+                    z = live[u]["z"][j, r]
+                    nc.vector.tensor_tensor(
+                        out=cell(inner, j, r), in0=z, in1=cell(inner, j, r), op=ALU.mult
+                    )
+                    nc.vector.scalar_tensor_tensor(
+                        out=cell(cube, j, r), in0=z, scalar=0.0, in1=cell(outer, j, r), op0=ALU.min, op1=ALU.mult
+                    )
             live[u]["cube"] = cube
-
-        def grouped_knots(u, value):
-            values = [value(g) for g in place(u)[1]]
-            if values[0] == values[1]:
-                return [(0, UNIT, values[0])]
-            return [(0, HALF, values[0]), (HALF, UNIT, values[1])]
 
         def stage_affine(u, columns):
             basis = work3.tile([P, UNIT], BF16, align_bytes=64)
-            one = columns[:, KNOTS : KNOTS + 1]
-            for first, last, sign in grouped_knots(u, lambda g: -1.0 if g == G - 1 else 1.0):
-                inner = live[u]["inner"][:, first:last]
-                if u == N_UNITS - 1:
-                    nc.scalar.activation(out=basis[:, first:last], in_=inner, func=ACT.Identity, bias=1.0, scale=sign)
-                else:
-                    nc.gpsimd.tensor_scalar(
-                        out=basis[:, first:last], in0=inner, scalar1=sign, scalar2=one, op0=ALU.mult, op1=ALU.add
+            inner = live[u]["inner"][:]
+            if u == N_UNITS - 1:
+                for j in range(KNOTS):
+                    nc.scalar.activation(
+                        out=half(basis, j), in_=half(inner, j), func=ACT.Identity, bias=-1.0, scale=-1.0
                     )
+            else:
+                nc.gpsimd.tensor_scalar(
+                    out=basis[:],
+                    in0=inner,
+                    scalar1=-1.0,
+                    scalar2=columns[:, KNOTS : KNOTS + 1],
+                    op0=ALU.mult,
+                    op1=ALU.add,
+                )
             live[u]["basis"] = basis
 
-        def stage_clamp(u):
-            cube = live[u]["cube"]
-            for first, last, factor in grouped_knots(
-                u, lambda g: 4.0 if g == G - 1 else -4.0 if by_max(u, g) else -2.0
-            ):
-                nc.vector.tensor_scalar(
-                    out=cube[:, first:last],
-                    in0=cube[:, first:last],
-                    scalar1=factor,
-                    scalar2=0.0,
-                    op0=ALU.mult,
-                    op1=ALU.max,
-                )
-
-        def stage_minimum(u):
-            basis = live[u]["basis"]
-            nc.vector.tensor_tensor(out=basis[:], in0=basis[:], in1=live[u]["cube"][:], op=ALU.min)
+        def stage_maximum(u, first=0, last=UNIT):
+            basis = live[u]["basis"][:, first:last]
+            nc.vector.tensor_tensor(out=basis, in0=basis, in1=live[u]["cube"][:, first:last], op=ALU.max)
 
         def stage_quantise(u):
             codes = queue.tile([P, KNOTS * CHUNK], U32, align_bytes=64)
             scales = queue.tile([P, KNOTS * CHUNK], U8, align_bytes=64)
-            nc.vector.quantize_mx(out=codes[:].bitcast(FP8X4), scales=scales[:], in_=live[u]["basis"][:])
+            if u < N_UNITS - 1:
+                nc.vector.quantize_mx(out=codes[:].bitcast(FP8X4), scales=scales[:], in_=live[u]["basis"][:])
+            else:
+                for j in range(KNOTS):
+                    stage_maximum(u, j * HALF, (j + 1) * HALF)
+                for j in range(KNOTS):
+                    here = slice(j * CHUNK, (j + 1) * CHUNK)
+                    nc.vector.quantize_mx(
+                        out=codes[:, here].bitcast(FP8X4), scales=scales[:, here], in_=half(live[u]["basis"], j)
+                    )
             live[u] = {"codes": codes, "scales": scales}
 
         def stage_matmul(u, j):
@@ -342,7 +386,7 @@ def tile_advancedkanlayer_pa_kernel(tc, x_norm, spline_weight, base_activation, 
         def store_chunk(c):
             for r in range(TILES):
                 total = work.tile([P, O], F32)
-                nc.vector.tensor_tensor(out=total[:], in0=acc[r][:], in1=base_tenth[c, r][:], op=ALU.add)
+                nc.vector.tensor_tensor(out=total[:], in0=base_tenth[c, r][:], in1=acc[r][:], op=ALU.subtract)
                 first = c * CHUNK + r * P
                 nc.sync.dma_start(out=out[first : first + P, :], in_=total[:])
 
@@ -358,10 +402,11 @@ def tile_advancedkanlayer_pa_kernel(tc, x_norm, spline_weight, base_activation, 
                 mybir.EngineType.Pool,
             }
         ):
+            halve_chunk(0, 0, nc.vector)
             stage_rows(0, knots_and_ones[:, 0, :])
-            halve_chunk(0, nc.vector)
             columns = hand_out(1)
             stage_rows(1, columns)
+            stage_halves(1)
             turn_chunk(0)
             copy_pair()
             stage_turn(0)
@@ -376,16 +421,19 @@ def tile_advancedkanlayer_pa_kernel(tc, x_norm, spline_weight, base_activation, 
                         stage_matmul(u, g % KNOTS)
                         progress["multiplied"] += 1
 
-            for k in range(N_UNITS + 3):
+            for k in range(N_UNITS + 4):
                 c, q = divmod(k, UNITS)
                 columns = hand_out(k + 2)
                 run(stage_affine, k - 1, columns)
-                if q == 0 and c + 1 < N_CHUNKS:
-                    halve_chunk(c + 1, nc.gpsimd)
+                if q in (0, UNITS - 1) and TURNING // UNITS <= c + 1 < N_CHUNKS:
+                    halve_chunk(c + 1, 0 if q == 0 else G - 1, nc.gpsimd)
                 run(stage_products, k)
+                if progress["multiplied"] == (progress["stored"] + 1) * G:
+                    store_chunk(progress["stored"])
+                    progress["stored"] += 1
                 copy_pair()
                 run(stage_turn, k + 1)
-                multiply(k - 1, k - 1, KNOTS)
+                multiply(k - 2, k - 1, KNOTS)
                 if k < TURNING:
                     turn_spline_weights(k, 0)
                     turn_spline_weights(k, 2)
@@ -395,21 +443,25 @@ def tile_advancedkanlayer_pa_kernel(tc, x_norm, spline_weight, base_activation, 
                 run(stage_rows, k + 2, columns)
                 copy_pair()
                 copy_pair()
-                run(stage_minimum, k - 1)
-                run(stage_clamp, k)
+                if k <= N_UNITS:
+                    run(stage_quantise, k - 2)
+                if k < N_UNITS:
+                    run(stage_maximum, k - 1)
+                elif k == N_UNITS:
+                    stage_quantise(k - 1)
+                if q == 0 and c < N_CHUNKS:
+                    negate_chunk(c)
+                if k + 2 < TURNING:
+                    run(stage_halves, k + 2)
                 if 1 <= k <= TURNING:
                     quantise_spline_weights(k - 1)
                 if k == TURNING:
                     quantise_base_weights()
-                if k >= TURNING and progress["based"] < min(c + 1, N_CHUNKS):
+                if k >= TURNING and progress["based"] < min(c + 1, progress["stored"] + 2, N_CHUNKS):
                     quantise_chunk(progress["based"])
                     base_product(progress["based"])
                     progress["based"] += 1
-                if progress["multiplied"] == (progress["stored"] + 1) * G:
-                    store_chunk(progress["stored"])
-                    progress["stored"] += 1
-                run(stage_quantise, k - 1)
-                multiply(k, k, 1)
+                multiply(k - 1 if k < N_UNITS else N_UNITS, k, 1 if k < N_UNITS else KNOTS)
                 if k in (1, 5):
                     turn_chunk(k // 4 + 1)
                 if k in (3, 7):

import math

import concourse.mybir as mybir
from concourse.masks import make_identity

F32 = mybir.dt.float32
BF16 = mybir.dt.bfloat16
U32 = mybir.dt.uint32
U8 = mybir.dt.uint8
FP8X4 = mybir.dt.float8_e4m3fn_x4
ACT = mybir.ActivationFunctionType
ALU = mybir.AluOpType

P = 128
PACK = 4
B, I, O, G = 2048, 512, 512, 8
TILES = 2
CHUNK = TILES * P
N_CHUNKS = B // CHUNK
O_TILES = O // P
KNOTS = 2
UNITS = G // KNOTS
CELL = P * PACK
HALF = TILES * CELL
UNIT = KNOTS * HALF
N_UNITS = N_CHUNKS * UNITS
TURNING = 8
SHARING = 3
HUGE = 3.0e38
ROOT12 = math.sqrt(12.0)

FLOPS = 2 * B * O * (I * G + I)


def tile_advancedkanlayer_pa_kernel(tc, x_norm, spline_weight, base_activation, grid_points, out):
    nc = tc.nc
    with tc.tile_pool(name="keep", bufs=1) as keep, tc.tile_pool(name="by_chunk", bufs=2) as by_chunk, tc.tile_pool(
        name="turned_x", bufs=4
    ) as turned_x, tc.tile_pool(name="work", bufs=2) as work, tc.tile_pool(name="work3", bufs=3) as work3, tc.tile_pool(
        name="queue", bufs=6
    ) as queue, tc.tile_pool(name="work4", bufs=4) as work4, tc.tile_pool(
        name="halves", bufs=5
    ) as halves, tc.psum_pool(name="psum_cells", bufs=KNOTS * TILES) as psum_cells, tc.psum_pool(
        name="psum_side", bufs=2
    ) as psum_side, tc.psum_pool(name="psum_acc", bufs=TILES) as psum_acc:
        ident = keep.tile([P, P], BF16)
        make_identity(nc, ident[:])
        ident_f32 = keep.tile([P, P], F32)
        make_identity(nc, ident_f32[:])

        x_sb = keep.tile([P, B // P, I], BF16)
        x_rows = x_norm.rearrange("(r p) i -> p r i", p=P)
        grid_bf = keep.tile([P, G], BF16)
        a_sb = keep.tile([P, O_TILES, I], BF16)
        w_sb = keep.tile([P, O_TILES, PACK, P, G], BF16)

        def load_x(first, last):
            nc.sync.dma_start(out=x_sb[:, first:last, :], in_=x_rows[:, first:last, :])

        load_x(0, TILES)
        nc.sync.dma_start(out=grid_bf[:], in_=grid_points.partition_broadcast(P))
        for s in range(O_TILES):
            nc.sync.dma_start(
                out=w_sb[:, s], in_=spline_weight[s * P : (s + 1) * P].rearrange("o (t q) g -> o t q g", t=PACK)
            )
            if s == 0:
                load_x(TILES, 2 * TILES)
        nc.sync.dma_start(out=a_sb[:], in_=base_activation.rearrange("(s p) i -> p s i", p=P))
        for r in range(2 * TILES, B // P, 4):
            load_x(r, min(r + 4, B // P))

        column_tiles = []

        def of_knots(factor, added):
            columns = keep.tile([P, G], F32, name="columns%d" % len(column_tiles))
            column_tiles.append(columns)
            nc.vector.tensor_scalar(
                out=columns[:], in0=grid_bf[:], scalar1=factor, scalar2=added, op0=ALU.mult, op1=ALU.add
            )
            return columns

        knots_and_ones = keep.tile([P, UNITS, KNOTS + 1], F32)
        nc.vector.memset(knots_and_ones[:], -1.0)
        nc.vector.tensor_copy(out=knots_and_ones[:, :, 0:KNOTS], in_=grid_bf[:].rearrange("p (q j) -> p q j", j=KNOTS))
        nc.vector.tensor_scalar(
            out=knots_and_ones[:, UNITS - 1, KNOTS - 1 : KNOTS],
            in0=grid_bf[:, G - 1 : G],
            scalar1=-1.0,
            scalar2=None,
            op0=ALU.mult,
        )
        minus_half_g = of_knots(-0.5, 0.0)
        minus_root12_g = of_knots(-ROOT12, 0.0)
        offset = of_knots(-0.5, -0.5)
        nc.vector.tensor_scalar(
            out=offset[:, G - 1 : G], in0=grid_bf[:, G - 1 : G], scalar1=0.5, scalar2=-0.5, op0=ALU.mult, op1=ALU.add
        )
        minus_half = keep.tile([P, P], F32)
        nc.vector.memset(minus_half[:], -0.5)
        half_step = keep.tile([P, P], F32)
        nc.vector.memset(half_step[:], 0.0)
        nc.vector.tensor_scalar(
            out=half_step[:],
            in0=half_step[:],
            scalar1=offset[:, SHARING : SHARING + 1],
            scalar2=offset[:, 0:1],
            op0=ALU.add,
            op1=ALU.subtract,
        )

        a_grouped = keep.tile([P, O, PACK], BF16, align_bytes=64)
        a_codes = keep.tile([P, O], U32, align_bytes=64)
        a_scales = keep.tile([P, O], U8, align_bytes=64)
        w_codes = keep.tile([P, G, O], U32, align_bytes=64)
        w_scales = keep.tile([P, G, O], U8, align_bytes=64)

        waiting = []

        def turn_pair(block, grouped):
            turned = psum_side.tile([P, 2, PACK, P], BF16, tag="side")
            for j in range(2):
                for t in range(PACK):
                    nc.tensor.transpose(out=turned[:, j, t, :], in_=block(j, t), identity=ident[:])
            waiting.append((turned, grouped))

        def copy_pair():
            if waiting:
                turned, grouped = waiting.pop(0)
                nc.scalar.copy(
                    out=grouped.rearrange("p (j r) t -> p j r t", j=2), in_=turned[:].rearrange("p j t r -> p j r t")
                )

        def quantise(codes, scales, grouped):
            nc.vector.quantize_mx(out=codes.bitcast(FP8X4), scales=scales, in_=grouped.rearrange("p n t -> p (n t)"))

        def turn_base_weights(s):
            turn_pair(lambda j, t: a_sb[:, s + j, t * P : (t + 1) * P], a_grouped[:, s * P : (s + 2) * P, :])

        def quantise_base_weights():
            quantise(a_codes[:], a_scales[:], a_grouped[:])

        w_turned = {}

        def turn_spline_weights(g, s):
            if s == 0:
                w_turned[g] = work.tile([P, O, PACK], BF16, align_bytes=64, name="w_grouped")
            turn_pair(lambda j, t: w_sb[:, s + j, t, :, g], w_turned[g][:, s * P : (s + 2) * P, :])

        def quantise_spline_weights(g):
            quantise(w_codes[:, g, :], w_scales[:, g, :], w_turned[g][:])

        x_turned = {}
        x_halved = {}
        x_negated = {}
        x_quantised = {}
        base_tenth = {}

        def turn_chunk(c):
            x_turned[c] = turned_x.tile([P, CHUNK, PACK], BF16, align_bytes=64, name="x_grouped")
            turn_pair(lambda j, t: x_sb[:, c * TILES + j, t * P : (t + 1) * P], x_turned[c][:])

        def halve_chunk(c, g, engine):
            x_halved[c, g] = halves.tile([P, TILES, I], F32, name="half_x")
            engine.tensor_scalar(
                out=x_halved[c, g][:],
                in0=x_sb[:, c * TILES : (c + 1) * TILES, :],
                scalar1=0.5 if g == G - 1 else -0.5,
                scalar2=offset[:, g : g + 1],
                op0=ALU.mult,
                op1=ALU.add,
            )

        def negate_chunk(c):
            x_negated[c] = by_chunk.tile([P, TILES, I], BF16, name="minus_x")
            nc.vector.tensor_scalar(
                out=x_negated[c][:],
                in0=x_sb[:, c * TILES : (c + 1) * TILES, :],
                scalar1=-1.0,
                scalar2=None,
                op0=ALU.mult,
            )

        def quantise_chunk(c):
            x_codes = by_chunk.tile([P, CHUNK], U32, align_bytes=64)
            x_scales = by_chunk.tile([P, CHUNK], U8, align_bytes=64)
            quantise(x_codes[:], x_scales[:], x_turned[c][:])
            x_quantised[c] = (x_codes, x_scales)

        def base_product(c):
            x_codes, x_scales = x_quantised[c]
            for r in range(TILES):
                rows = slice(r * P, (r + 1) * P)
                base_ps = psum_side.tile([P, O], F32, tag="side")
                nc.tensor.matmul_mx(
                    out=base_ps[:],
                    lhsT=x_codes[:, rows].bitcast(FP8X4),
                    lhsT_scale=x_scales[:, rows],
                    rhs=a_codes[:].bitcast(FP8X4),
                    rhs_scale=a_scales[:],
                    start=True,
                    stop=True,
                )
                tenth = work4.tile([P, O], F32)
                nc.scalar.mul(out=tenth[:], in_=base_ps[:], mul=0.1)
                base_tenth[c, r] = tenth

        def keep_clock():
            unread = psum_side.tile([P, P], F32, tag="side")
            nc.tensor.matmul(out=unread[:], lhsT=ident_f32[:], rhs=ident_f32[:], start=True, stop=True)

        live = {}
        acc = {}

        def place(u):
            c, q = divmod(u, UNITS)
            return c, range(q * KNOTS, (q + 1) * KNOTS)

        def by_max(u, g):
            return g in (0, G - 1) or (g % KNOTS == 0 if u < TURNING else g == SHARING)

        def addends(u, g):
            c, knots = place(u)
            rows = live[u]["rows"]
            parts = [lambda r, features: rows[:, g - knots[0], r, features]]
            if not by_max(u, g):
                return parts + [lambda r, features: minus_half[:]]
            if (c, g) in x_halved:
                return parts + [lambda r, features: x_halved[c, g][:, r, features]]
            return parts + [lambda r, features: x_halved[c, 0][:, r, features], lambda r, features: half_step[:]]

        def half(tile, j):
            return tile[:, j * HALF : (j + 1) * HALF]

        def cell(tile, j, r):
            start = j * HALF + r * CELL
            return tile[:, start : start + CELL].rearrange("p (b t) -> p b t", t=PACK)

        def hand_out(u):
            columns = work.tile([P, KNOTS + 1], F32)
            nc.vector.tensor_copy(out=columns[:], in_=knots_and_ones[:, u % UNITS, :])
            return columns

        def stage_rows(u, columns):
            c, knots = place(u)
            engine = nc.vector if u == 0 else nc.gpsimd
            x_here = x_sb[:, c * TILES : (c + 1) * TILES, :]
            rows = work3.tile([P, KNOTS, TILES, I], F32)
            for j, g in enumerate(knots):
                if by_max(u, g):
                    engine.tensor_scalar(
                        out=rows[:, j],
                        in0=x_negated[c][:] if g == G - 1 else x_here,
                        scalar1=HUGE,
                        scalar2=columns[:, j : j + 1],
                        op0=ALU.min,
                        op1=ALU.max,
                    )
                else:
                    nc.scalar.activation(
                        out=rows[:, j], in_=x_here, func=ACT.Abs, bias=minus_half_g[:, g : g + 1], scale=0.5
                    )
            live[u] = {"rows": rows}

        def stage_halves(u):
            c, knots = place(u)
            for g in knots:
                if by_max(u, g):
                    halve_chunk(c, g, nc.vector)

        def stage_turn(u):
            c, knots = place(u)
            live[u]["z"] = {}
            for j, g in enumerate(knots):
                parts = addends(u, g)
                for r in range(TILES):
                    z = psum_cells.tile([P, PACK, P], F32)
                    for t in range(PACK):
                        for i, part in enumerate(parts):
                            nc.tensor.matmul(
                                out=z[:, t, :],
                                lhsT=part(r, slice(t * P, (t + 1) * P)),
                                rhs=ident_f32[:],
                                is_transpose=True,
                                start=i == 0,
                                stop=i + 1 == len(parts),
                            )
                    live[u]["z"][j, r] = z[:].rearrange("p t b -> p b t")
                    keep_clock()

        def stage_squares(u):
            c, knots = place(u)
            inner = work3.tile([P, UNIT], F32)
            outer = work.tile([P, UNIT], F32)
            x_here = x_turned[c][:].rearrange("p b t -> p (b t)")

            def outer_square(j, r):
                nc.scalar.activation(out=cell(outer, j, r), in_=live[u]["z"][j, r], func=ACT.Square, scale=4.0)

            def inner_square(j):
                g = knots[j]
                nc.scalar.activation(
                    out=half(inner, j), in_=x_here, func=ACT.Square, bias=minus_root12_g[:, g : g + 1], scale=ROOT12
                )

            if u == 0:
                inner_square(0)
            outer_square(0, 0)
            if u > 0:
                inner_square(0)
            outer_square(0, 1)
            inner_square(1)
            outer_square(1, 0)
            outer_square(1, 1)
            live[u]["inner"] = inner
            live[u]["outer"] = outer

        def stage_products(u):
            inner, outer = live[u]["inner"], live[u]["outer"]
            cube = work.tile([P, UNIT], BF16, align_bytes=64)
            for j in range(KNOTS):
                for r in range(TILES):
                    z = live[u]["z"][j, r]
                    nc.vector.tensor_tensor(
                        out=cell(inner, j, r), in0=z, in1=cell(inner, j, r), op=ALU.mult
                    )
                    nc.vector.scalar_tensor_tensor(
                        out=cell(cube, j, r), in0=z, scalar=0.0, in1=cell(outer, j, r), op0=ALU.min, op1=ALU.mult
                    )
            live[u]["cube"] = cube

        def stage_affine(u, columns):
            basis = work3.tile([P, UNIT], BF16, align_bytes=64)
            inner = live[u]["inner"][:]
            if u == N_UNITS - 1:
                for j in range(KNOTS):
                    nc.scalar.activation(
                        out=half(basis, j), in_=half(inner, j), func=ACT.Identity, bias=-1.0, scale=-1.0
                    )
            else:
                nc.gpsimd.tensor_scalar(
                    out=basis[:],
                    in0=inner,
                    scalar1=-1.0,
                    scalar2=columns[:, KNOTS : KNOTS + 1],
                    op0=ALU.mult,
                    op1=ALU.add,
                )
            live[u]["basis"] = basis

        def stage_maximum(u, first=0, last=UNIT):
            basis = live[u]["basis"][:, first:last]
            nc.vector.tensor_tensor(out=basis, in0=basis, in1=live[u]["cube"][:, first:last], op=ALU.max)

        def stage_quantise(u):
            codes = queue.tile([P, KNOTS * CHUNK], U32, align_bytes=64)
            scales = queue.tile([P, KNOTS * CHUNK], U8, align_bytes=64)
            if u < N_UNITS - 1:
                nc.vector.quantize_mx(out=codes[:].bitcast(FP8X4), scales=scales[:], in_=live[u]["basis"][:])
            else:
                for j in range(KNOTS):
                    stage_maximum(u, j * HALF, (j + 1) * HALF)
                for j in range(KNOTS):
                    here = slice(j * CHUNK, (j + 1) * CHUNK)
                    nc.vector.quantize_mx(
                        out=codes[:, here].bitcast(FP8X4), scales=scales[:, here], in_=half(live[u]["basis"], j)
                    )
            live[u] = {"codes": codes, "scales": scales}

        def stage_matmul(u, j):
            codes, scales = live[u]["codes"], live[u]["scales"]
            for g in place(u)[1][j : j + 1]:
                for r in range(TILES):
                    if g == 0:
                        acc[r] = psum_acc.tile([P, O], F32, name="acc")
                    rows = slice(j * CHUNK + r * P, j * CHUNK + (r + 1) * P)
                    nc.tensor.matmul_mx(
                        out=acc[r][:],
                        lhsT=codes[:, rows].bitcast(FP8X4),
                        lhsT_scale=scales[:, rows],
                        rhs=w_codes[:, g, :].bitcast(FP8X4),
                        rhs_scale=w_scales[:, g, :],
                        start=(g == 0),
                        stop=(g == G - 1),
                    )

        def store_chunk(c):
            for r in range(TILES):
                total = work.tile([P, O], F32)
                nc.vector.tensor_tensor(out=total[:], in0=base_tenth[c, r][:], in1=acc[r][:], op=ALU.subtract)
                first = c * CHUNK + r * P
                nc.sync.dma_start(out=out[first : first + P, :], in_=total[:])

        def run(stage, u, *others):
            if 0 <= u < N_UNITS:
                stage(u, *others)

        with tc.manual_schedule(
            engines={
                mybir.EngineType.PE,
                mybir.EngineType.Activation,
                mybir.EngineType.DVE,
                mybir.EngineType.Pool,
            }
        ):
            halve_chunk(0, 0, nc.vector)
            stage_rows(0, knots_and_ones[:, 0, :])
            columns = hand_out(1)
            stage_rows(1, columns)
            stage_halves(1)
            turn_chunk(0)
            copy_pair()
            stage_turn(0)
            stage_squares(0)
            progress = {"multiplied": 0, "stored": 0, "based": 0}

            def multiply(quantised, weighed, most):
                for n in range(most):
                    c, g = divmod(progress["multiplied"], G)
                    u = progress["multiplied"] // KNOTS
                    if u < min(quantised, N_UNITS) and (c > 0 or g < weighed) and c == progress["stored"]:
                        stage_matmul(u, g % KNOTS)
                        progress["multiplied"] += 1

            for k in range(N_UNITS + 4):
                c, q = divmod(k, UNITS)
                columns = hand_out(k + 2)
                run(stage_affine, k - 1, columns)
                if q in (0, UNITS - 1) and TURNING // UNITS <= c + 1 < N_CHUNKS:
                    halve_chunk(c + 1, 0 if q == 0 else G - 1, nc.gpsimd)
                run(stage_products, k)
                if progress["multiplied"] == (progress["stored"] + 1) * G:
                    store_chunk(progress["stored"])
                    progress["stored"] += 1
                copy_pair()
                run(stage_turn, k + 1)
                multiply(k - 2, k - 1, KNOTS)
                if k < TURNING:
                    turn_spline_weights(k, 0)
                    turn_spline_weights(k, 2)
                elif q == 1 and c + 1 < N_CHUNKS:
                    turn_chunk(c + 1)
                run(stage_squares, k + 1)
                run(stage_rows, k + 2, columns)
                copy_pair()
                copy_pair()
                if k <= N_UNITS:
                    run(stage_quantise, k - 2)
                if k < N_UNITS:
                    run(stage_maximum, k - 1)
                elif k == N_UNITS:
                    stage_quantise(k - 1)
                if q == 0 and c < N_CHUNKS:
                    negate_chunk(c)
                if k + 2 < TURNING:
                    run(stage_halves, k + 2)
                if 1 <= k <= TURNING:
                    quantise_spline_weights(k - 1)
                if k == TURNING:
                    quantise_base_weights()
                if k >= TURNING and progress["based"] < min(c + 1, progress["stored"] + 2, N_CHUNKS):
                    quantise_chunk(progress["based"])
                    base_product(progress["based"])
                    progress["based"] += 1
                multiply(k - 1 if k < N_UNITS else N_UNITS, k, 1 if k < N_UNITS else KNOTS)
                if k in (1, 5):
                    turn_chunk(k // 4 + 1)
                if k in (3, 7):
                    turn_base_weights(k // 4 * 2)
            if progress["stored"] < N_CHUNKS:
                store_chunk(progress["stored"])
